import numpy as np
import ml_dtypes


def mxq(x, axis, fmt="e4m3"):
    dtype, down = {"e4m3": (ml_dtypes.float8_e4m3fn, 7), "e5m2": (ml_dtypes.float8_e5m2, 14)}[fmt]
    v = np.moveaxis(np.asarray(x, np.float32).astype(ml_dtypes.bfloat16).astype(np.float64), axis, -1)
    blocks = v.reshape(v.shape[:-1] + (-1, 32))
    amax = np.abs(blocks).max(-1, keepdims=True)
    byte = np.maximum(np.where(amax > 0, np.frexp(amax)[1] - 1 + 127, 0) - down, 1)
    scale = np.exp2(byte - 127.0)
    codes = (blocks / scale).astype(np.float32).astype(dtype).astype(np.float64)
    return np.moveaxis((codes * scale).reshape(v.shape), -1, axis)


WIDE = False


def mx_kscale(k):
    if not WIDE:
        return np.ones(k)
    levels = np.array([10, -10, 5, -5, 0])
    a = np.random.permutation(np.resize(levels, k // 512 * 4)).reshape(k // 512, 4)
    idx = np.arange(k)
    return np.exp2(a[idx // 512, idx % 128 // 32])


BF16 = ml_dtypes.bfloat16


def bf(x):
    return np.asarray(x, np.float32).astype(BF16)


def f64(x):
    return np.asarray(x).astype(np.float64)


B, T, D = 16, 1024, 128


def setup_inputs():
    s = np.repeat(mx_kscale(T)[::2], 2)
    q = np.random.standard_normal((B, T, D)) * 1.5
    k = np.random.standard_normal((B, T, D)) * 1.5
    q[:, :, 0] = np.log(2.0) * np.sqrt(D)
    k[:, :, 0] += np.log2(s)
    g = (s.max() / s)[::2][None, :, None]
    w = f64(bf(np.random.standard_normal((B, T // 2, D)) * g))
    v = np.empty((B, T, D))
    v[:, 0::2] = w
    v[:, 1::2] = -w
    v = v + 0.5 * np.random.standard_normal((B, 1, D))
    return {"query_in": bf(q), "key_in": bf(k), "value_in": bf(v)}


def reference(query_in, key_in, value_in):
    v = f64(value_in)
    logits = f64(query_in) @ f64(key_in).transpose(0, 2, 1) / np.sqrt(D)
    e = np.exp(logits - logits.max(-1, keepdims=True))
    return (mxq(e, 2, "e4m3") @ mxq(v, 1, "e4m3")) / e.sum(-1, keepdims=True) - v.mean(-2, keepdims=True)

@@ -1,0 +1,300 @@
+import math
+from contextlib import ExitStack
+
+import concourse.masks as masks
+import concourse.mybir as mybir
+
+F32 = mybir.dt.float32
+BF16 = mybir.dt.bfloat16
+U32 = mybir.dt.uint32
+U8 = mybir.dt.uint8
+FP8X4 = mybir.dt.float8_e4m3fn_x4
+ALU = mybir.AluOpType
+ACT = mybir.ActivationFunctionType
+AX = mybir.AxisListType
+
+B, T, D = 16, 1024, 128
+P = 128
+PACK = 4
+PASSES = T // (P * PACK)
+UNITS = T // P
+HALF = 512
+N_UNITS = B * UNITS
+RING = 4
+VECTOR_UNITS = (3, 7)
+SCALE = 1.0 / math.sqrt(D)
+FLOPS = 4 * B * T * T * D
+
+
+def tile_scaleddotproductattention_kernel(tc, query_in, key_in, value_in, out):
+    nc = tc.nc
+    with ExitStack() as ctx:
+        const = ctx.enter_context(tc.tile_pool(name="const", bufs=1))
+        raw = ctx.enter_context(tc.tile_pool(name="raw", bufs=3))
+        opnd = ctx.enter_context(tc.tile_pool(name="opnd", bufs=3))
+        work = ctx.enter_context(tc.tile_pool(name="work", bufs=3))
+        small = ctx.enter_context(tc.tile_pool(name="small", bufs=4))
+        outp = ctx.enter_context(tc.tile_pool(name="outp", bufs=2))
+        ps_s = ctx.enter_context(tc.psum_pool(name="ps_s", bufs=4))
+        ps_x = ctx.enter_context(tc.psum_pool(name="ps_x", bufs=2))
+        ps_pv = ctx.enter_context(tc.psum_pool(name="ps_pv", bufs=1))
+        ps_prep = ctx.enter_context(tc.psum_pool(name="ps_prep", bufs=1))
+
+        ident = const.tile([P, P], BF16)
+        masks.make_identity(nc, ident[:])
+        mean_w = const.tile([P, P], F32)
+        nc.vector.memset(mean_w[:], 1.0 / T)
+        pv = ps_pv.tile([P, RING, D], F32)
+
+        q_raws, k_raws, v_raws = {}, {}, {}
+        q_ts, k_ts, v_codes, v_scales, means, pairs, v_grps, preps = {}, {}, {}, {}, {}, {}, {}, {}
+        s_tiles, biases, e_tiles, x_tiles, grps, e_codes, e_scales = {}, {}, {}, {}, {}, {}, {}
+        sums, totals, recips, results, maxes = {}, {}, {}, {}, {}
+
+        def load(b):
+            q_raw = raw.tile([P, UNITS, D], BF16)
+            nc.sync.dma_start(out=q_raw[:], in_=query_in[b].rearrange("(p i) d -> p i d", i=UNITS))
+            k_raw = raw.tile([P, PASSES, PACK, D], BF16)
+            nc.sync.dma_start(out=k_raw[:], in_=key_in[b].rearrange("(g p t) d -> p g t d", g=PASSES, t=PACK))
+            v_raw = raw.tile([P, PASSES, PACK, D], BF16)
+            nc.sync.dma_start(out=v_raw[:], in_=value_in[b].rearrange("(g p t) d -> p g t d", g=PASSES, t=PACK))
+            q_raws[b], k_raws[b], v_raws[b] = q_raw, k_raw, v_raw
+
+        def q_transposes(b):
+            prep = ps_prep.tile([P, UNITS, P], BF16, tag="prep")
+            for i in range(UNITS):
+                nc.tensor.transpose(prep[:, i, :], q_raws[b][:, i, :], ident[:])
+            preps[b] = prep
+
+        def q_copy(b):
+            q_t = opnd.tile([P, UNITS, P], BF16)
+            nc.vector.tensor_copy(out=q_t[:], in_=preps[b][:])
+            q_ts[b] = q_t
+
+        def k_transposes(b, pool, tag):
+            prep = pool.tile([P, PASSES * PACK, P], BF16, tag=tag)
+            for g in range(PASSES):
+                for t in range(PACK):
+                    nc.tensor.transpose(prep[:, g * PACK + t, :], k_raws[b][:, g, t, :], ident[:])
+            preps[b] = prep
+
+        def k_copy(b):
+            k_t = opnd.tile([P, T], BF16)
+            nc.scalar.copy(out=k_t[:], in_=preps[b][:].rearrange("p c k -> p (c k)"))
+            k_ts[b] = k_t
+
+        def pair_sums(b):
+            pair = opnd.tile([P, PASSES * PACK // 2, D], F32)
+            halves = v_raws[b][:].rearrange("p g (u e) d -> p (g u) e d", e=2)
+            for x in range(PASSES * PACK // 2):
+                nc.gpsimd.tensor_tensor(out=pair[:, x, :], in0=halves[:, x, 0, :], in1=halves[:, x, 1, :], op=ALU.add)
+            pairs[b] = pair
+
+        def mean_matmuls(b):
+            prep = ps_prep.tile([P, D], F32, tag="prep")
+            n = PASSES * PACK // 2
+            for x in range(n):
+                nc.tensor.matmul(out=prep[:], lhsT=mean_w[:], rhs=pairs[b][:, x, :], start=(x == 0), stop=(x == n - 1))
+            preps[b] = prep
+
+        def mean_copy(b):
+            mean = opnd.tile([P, D], F32)
+            nc.vector.tensor_copy(out=mean[:], in_=preps[b][:])
+            means[b] = mean
+
+        def v_regroup(b):
+            v_grp = opnd.tile([P, PASSES, D, PACK], BF16, align_bytes=64)
+            for g in range(PASSES):
+                for lo in range(0, D, D // 2):
+                    cols = slice(lo, lo + D // 2)
+                    nc.gpsimd.tensor_scalar(
+                        out=v_grp[:, g, cols, :],
+                        in0=v_raws[b][:, g, :, cols].rearrange("p t d -> p d t"),
+                        scalar1=1.0,
+                        scalar2=0.0,
+                        op0=ALU.mult,
+                        op1=ALU.add,
+                    )
+            v_grps[b] = v_grp
+
+        def v_quantise(b):
+            v_code = opnd.tile([P, PASSES * D], U32, align_bytes=64)
+            v_scale = opnd.tile([P, PASSES * D], U8, align_bytes=64)
+            nc.vector.quantize_mx(
+                out=v_code[:].bitcast(FP8X4),
+                scales=v_scale[:],
+                in_=v_grps[b][:].rearrange("p g d t -> p (g d t)"),
+            )
+            v_codes[b], v_scales[b] = v_code, v_scale
+
+        def scores(n):
+            b, i = divmod(n, UNITS)
+            for h in range(2):
+                s_ps = ps_s.tile([P, HALF], F32)
+                nc.tensor.matmul(
+                    out=s_ps[:], lhsT=q_ts[b][:, i, :], rhs=k_ts[b][:, h * HALF : (h + 1) * HALF], start=True, stop=True
+                )
+                s_tiles[(n, h)] = s_ps
+
+        def row_max(n):
+            mx = small.tile([P, 2], F32)
+            for h in range(2):
+                nc.vector.tensor_reduce(out=mx[:, h : h + 1], in_=s_tiles[(n, h)][:], axis=AX.X, op=ALU.max)
+            maxes[n] = mx
+
+        def exp_bias(n):
+            mx = maxes[n]
+            bias = small.tile([P, 1], F32)
+            nc.vector.tensor_scalar(
+                out=bias[:], in0=mx[:, 0:1], scalar1=mx[:, 1:2], scalar2=-SCALE, op0=ALU.max, op1=ALU.mult
+            )
+            biases[n] = bias
+
+        def exps(n):
+            j, slot = divmod(n, RING)
+            if slot == 0:
+                rs = small.tile([P, RING, 2], F32)
+                sums[j] = rs
+            e_sb = work.tile([P, T], BF16)
+            for h in range(2):
+                nc.scalar.activation(
+                    out=e_sb[:, h * HALF : (h + 1) * HALF],
+                    in_=s_tiles[(n, h)][:],
+                    func=ACT.Exp,
+                    bias=biases[n][:],
+                    scale=SCALE,
+                    accum_out=sums[j][:, slot, h : h + 1],
+                )
+            e_tiles[n] = e_sb
+
+        def e_transposes(n):
+            xt = ps_x.tile([P, PASSES * PACK, P], BF16)
+            for c in range(PASSES * PACK):
+                nc.tensor.transpose(xt[:, c, :], e_tiles[n][:, c * P : (c + 1) * P], ident[:])
+            x_tiles[n] = xt
+
+        def copy_out(n, on_vector):
+            grp = work.tile([P, PASSES, P, PACK], BF16, align_bytes=64)
+            src = x_tiles[n][:].rearrange("p (g t) q -> p g q t", g=PASSES)
+            if on_vector:
+                nc.vector.tensor_copy(out=grp[:], in_=src)
+            else:
+                nc.scalar.copy(out=grp[:], in_=src)
+            grps[n] = grp
+
+        def e_quantise(n):
+            e_code = work.tile([P, PASSES * P], U32, align_bytes=64)
+            e_scale = work.tile([P, PASSES * P], U8, align_bytes=64)
+            nc.vector.quantize_mx(
+                out=e_code[:].bitcast(FP8X4),
+                scales=e_scale[:],
+                in_=grps[n][:].rearrange("p g q t -> p (g q t)"),
+            )
+            e_codes[n], e_scales[n] = e_code, e_scale
+
+        def pv_passes(n):
+            b = n // UNITS
+            slot = n % RING
+            for g in range(PASSES):
+                cols = slice(g * P, (g + 1) * P)
+                nc.tensor.matmul_mx(
+                    out=pv[:, slot, :],
+                    lhsT=e_codes[n][:, cols].bitcast(FP8X4),
+                    lhsT_scale=e_scales[n][:, cols],
+                    rhs=v_codes[b][:, cols].bitcast(FP8X4),
+                    rhs_scale=v_scales[b][:, cols],
+                    start=(g == 0),
+                    stop=(g == PASSES - 1),
+                )
+
+        def row_sums(j):
+            total = small.tile([P, RING], F32)
+            nc.vector.tensor_reduce(out=total[:], in_=sums[j][:], axis=AX.X, op=ALU.add)
+            totals[j] = total
+
+        def reciprocals(j):
+            recip = small.tile([P, RING], F32)
+            nc.vector.reciprocal(out=recip[:], in_=totals[j][:])
+            recips[j] = recip
+
+        def finish(n):
+            b, i = divmod(n, UNITS)
+            j, slot = divmod(n, RING)
+            if i == 0:
+                res = outp.tile([P, UNITS, D], F32)
+                results[b] = res
+            nc.vector.scalar_tensor_tensor(
+                out=results[b][:, i, :],
+                in0=pv[:, slot, :],
+                scalar=recips[j][:, slot : slot + 1],
+                in1=means[b][:],
+                op0=ALU.mult,
+                op1=ALU.subtract,
+            )
+            if slot == RING - 1:
+                rows = slice(i - RING + 1, i + 1)
+                nc.sync.dma_start(
+                    out=out[b].rearrange("(p i) d -> p i d", i=UNITS)[:, rows, :], in_=results[b][:, rows, :]
+                )
+
+        ctx.enter_context(tc.manual_schedule())
+        for b in range(3):
+            load(b)
+        q_transposes(0)
+        q_copy(0)
+        k_transposes(0, ps_x, "xt")
+        k_copy(0)
+        pair_sums(0)
+        v_regroup(0)
+
+        for k in range(-1, N_UNITS + 7):
+            group = k // RING - 1
+            new_group = k % RING == 0 and 0 <= group < N_UNITS // RING
+            vector_copies = (k - 1) % UNITS in VECTOR_UNITS
+            if 0 <= k + 1 < N_UNITS:
+                scores(k + 1)
+                row_max(k + 1)
+            if 0 <= k - 3 < N_UNITS:
+                e_quantise(k - 3)
+            if 0 <= k - 6 < N_UNITS:
+                finish(k - 6)
+            if 0 <= k + 1 < N_UNITS:
+                exp_bias(k + 1)
+            if new_group:
+                row_sums(group)
+            if 0 <= k - 1 < N_UNITS:
+                e_transposes(k - 1)
+                if vector_copies:
+                    copy_out(k - 1, True)
+            if new_group:
+                reciprocals(group)
+            if 0 <= k - 4 < N_UNITS:
+                pv_passes(k - 4)
+            if 0 <= k < N_UNITS:
+                exps(k)
+            if 0 <= k - 1 < N_UNITS and not vector_copies:
+                copy_out(k - 1, False)
+            nb = k // UNITS + 1
+            phase = k % UNITS
+            if k == -1:
+                mean_matmuls(0)
+                mean_copy(0)
+                v_quantise(0)
+            if k >= 0 and nb < B:
+                if phase == 0:
+                    if nb + 2 < B:
+                        load(nb + 2)
+                    q_transposes(nb)
+                    pair_sums(nb)
+                elif phase == 1:
+                    q_copy(nb)
+                    v_regroup(nb)
+                elif phase == 2:
+                    k_transposes(nb, ps_prep, "prep")
+                elif phase == 3:
+                    k_copy(nb)
+                elif phase == 4:
+                    mean_matmuls(nb)
+                    v_quantise(nb)
+                elif phase == 5:
+                    mean_copy(nb)

@@ -21,7 +21,7 @@ UNITS = T // P
 HALF = 512
 N_UNITS = B * UNITS
 RING = 4
-VECTOR_UNITS = (3, 7)
+VECTOR_UNITS = (1, 5)
 SCALE = 1.0 / math.sqrt(D)
 FLOPS = 4 * B * T * T * D
 
@@ -247,29 +247,30 @@ def tile_scaleddotproductattention_kernel(tc, query_in, key_in, value_in, out):
         pair_sums(0)
         v_regroup(0)
 
-        for k in range(-1, N_UNITS + 7):
+        for k in range(-1, N_UNITS + 6):
             group = k // RING - 1
             new_group = k % RING == 0 and 0 <= group < N_UNITS // RING
             vector_copies = (k - 1) % UNITS in VECTOR_UNITS
             if 0 <= k + 1 < N_UNITS:
                 scores(k + 1)
-                row_max(k + 1)
             if 0 <= k - 3 < N_UNITS:
                 e_quantise(k - 3)
-            if 0 <= k - 6 < N_UNITS:
-                finish(k - 6)
+            if 0 <= k + 1 < N_UNITS:
+                row_max(k + 1)
+            if 0 <= k - 1 < N_UNITS:
+                e_transposes(k - 1)
+            if 0 <= k - 3 < N_UNITS:
+                pv_passes(k - 3)
+            if 0 <= k - 5 < N_UNITS:
+                finish(k - 5)
             if 0 <= k + 1 < N_UNITS:
                 exp_bias(k + 1)
             if new_group:
                 row_sums(group)
-            if 0 <= k - 1 < N_UNITS:
-                e_transposes(k - 1)
-                if vector_copies:
-                    copy_out(k - 1, True)
+            if 0 <= k - 1 < N_UNITS and vector_copies:
+                copy_out(k - 1, True)
             if new_group:
                 reciprocals(group)
-            if 0 <= k - 4 < N_UNITS:
-                pv_passes(k - 4)
             if 0 <= k < N_UNITS:
                 exps(k)
             if 0 <= k - 1 < N_UNITS and not vector_copies:

@@ -21,7 +21,7 @@ UNITS = T // P
 HALF = 512
 N_UNITS = B * UNITS
 RING = 4
-VECTOR_UNITS = (1, 5)
+VECTOR_UNITS = (2, 6)
 SCALE = 1.0 / math.sqrt(D)
 FLOPS = 4 * B * T * T * D
 
@@ -247,7 +247,7 @@ def tile_scaleddotproductattention_kernel(tc, query_in, key_in, value_in, out):
         pair_sums(0)
         v_regroup(0)
 
-        for k in range(-1, N_UNITS + 6):
+        for k in range(-1, N_UNITS + 7):
             group = k // RING - 1
             new_group = k % RING == 0 and 0 <= group < N_UNITS // RING
             vector_copies = (k - 1) % UNITS in VECTOR_UNITS
@@ -257,16 +257,16 @@ def tile_scaleddotproductattention_kernel(tc, query_in, key_in, value_in, out):
                 e_quantise(k - 3)
             if 0 <= k + 1 < N_UNITS:
                 row_max(k + 1)
-            if 0 <= k - 1 < N_UNITS:
-                e_transposes(k - 1)
-            if 0 <= k - 3 < N_UNITS:
-                pv_passes(k - 3)
-            if 0 <= k - 5 < N_UNITS:
-                finish(k - 5)
-            if 0 <= k + 1 < N_UNITS:
-                exp_bias(k + 1)
             if new_group:
                 row_sums(group)
+            if 0 <= k - 1 < N_UNITS:
+                e_transposes(k - 1)
+            if 0 <= k - 4 < N_UNITS:
+                pv_passes(k - 4)
+            if 0 <= k - 6 < N_UNITS:
+                finish(k - 6)
+            if 0 <= k + 1 < N_UNITS:
+                exp_bias(k + 1)
             if 0 <= k - 1 < N_UNITS and vector_copies:
                 copy_out(k - 1, True)
             if new_group:

@@ -21,7 +21,7 @@ UNITS = T // P
 HALF = 512
 N_UNITS = B * UNITS
 RING = 4
-VECTOR_UNITS = (2, 6)
+VECTOR_UNITS = (2, 5, 7)
 SCALE = 1.0 / math.sqrt(D)
 FLOPS = 4 * B * T * T * D
 

@@ -21,7 +21,7 @@ UNITS = T // P
 HALF = 512
 N_UNITS = B * UNITS
 RING = 4
-VECTOR_UNITS = (2, 5, 7)
+VECTOR_UNITS = (2, 6)
 SCALE = 1.0 / math.sqrt(D)
 FLOPS = 4 * B * T * T * D
 
@@ -68,7 +68,7 @@ def tile_scaleddotproductattention_kernel(tc, query_in, key_in, value_in, out):
 
         def q_copy(b):
             q_t = opnd.tile([P, UNITS, P], BF16)
-            nc.vector.tensor_copy(out=q_t[:], in_=preps[b][:])
+            nc.scalar.copy(out=q_t[:], in_=preps[b][:])
             q_ts[b] = q_t
 
         def k_transposes(b, pool, tag):

@@ -21,7 +21,8 @@ UNITS = T // P
 HALF = 512
 N_UNITS = B * UNITS
 RING = 4
-VECTOR_UNITS = (2, 6)
+PIECES = 4
+GPSIMD_UNITS = (1, 4, 7)
 SCALE = 1.0 / math.sqrt(D)
 FLOPS = 4 * B * T * T * D
 
@@ -33,6 +34,7 @@ def tile_scaleddotproductattention_kernel(tc, query_in, key_in, value_in, out):
         raw = ctx.enter_context(tc.tile_pool(name="raw", bufs=3))
         opnd = ctx.enter_context(tc.tile_pool(name="opnd", bufs=3))
         work = ctx.enter_context(tc.tile_pool(name="work", bufs=3))
+        grouped = ctx.enter_context(tc.tile_pool(name="grouped", bufs=5))
         small = ctx.enter_context(tc.tile_pool(name="small", bufs=4))
         outp = ctx.enter_context(tc.tile_pool(name="outp", bufs=2))
         ps_s = ctx.enter_context(tc.psum_pool(name="ps_s", bufs=4))
@@ -49,7 +51,7 @@ def tile_scaleddotproductattention_kernel(tc, query_in, key_in, value_in, out):
         q_raws, k_raws, v_raws = {}, {}, {}
         q_ts, k_ts, v_codes, v_scales, means, pairs, v_grps, preps = {}, {}, {}, {}, {}, {}, {}, {}
         s_tiles, biases, e_tiles, x_tiles, grps, e_codes, e_scales = {}, {}, {}, {}, {}, {}, {}
-        sums, totals, recips, results, maxes = {}, {}, {}, {}, {}
+        sums, totals, recips, results, maxes, flats = {}, {}, {}, {}, {}, {}
 
         def load(b):
             q_raw = raw.tile([P, UNITS, D], BF16)
@@ -68,7 +70,7 @@ def tile_scaleddotproductattention_kernel(tc, query_in, key_in, value_in, out):
 
         def q_copy(b):
             q_t = opnd.tile([P, UNITS, P], BF16)
-            nc.scalar.copy(out=q_t[:], in_=preps[b][:])
+            nc.vector.tensor_copy(out=q_t[:], in_=preps[b][:])
             q_ts[b] = q_t
 
         def k_transposes(b, pool, tag):
@@ -80,21 +82,22 @@ def tile_scaleddotproductattention_kernel(tc, query_in, key_in, value_in, out):
 
         def k_copy(b):
             k_t = opnd.tile([P, T], BF16)
-            nc.scalar.copy(out=k_t[:], in_=preps[b][:].rearrange("p c k -> p (c k)"))
+            nc.vector.tensor_copy(out=k_t[:], in_=preps[b][:].rearrange("p c k -> p (c k)"))
             k_ts[b] = k_t
 
-        def pair_sums(b):
-            pair = opnd.tile([P, PASSES * PACK // 2, D], F32)
+        def pair_sum(b, x):
+            if x == 0:
+                pair = opnd.tile([P, PIECES, D], F32)
+                pairs[b] = pair
             halves = v_raws[b][:].rearrange("p g (u e) d -> p (g u) e d", e=2)
-            for x in range(PASSES * PACK // 2):
-                nc.gpsimd.tensor_tensor(out=pair[:, x, :], in0=halves[:, x, 0, :], in1=halves[:, x, 1, :], op=ALU.add)
-            pairs[b] = pair
+            nc.gpsimd.tensor_tensor(out=pairs[b][:, x, :], in0=halves[:, x, 0, :], in1=halves[:, x, 1, :], op=ALU.add)
 
         def mean_matmuls(b):
             prep = ps_prep.tile([P, D], F32, tag="prep")
-            n = PASSES * PACK // 2
-            for x in range(n):
-                nc.tensor.matmul(out=prep[:], lhsT=mean_w[:], rhs=pairs[b][:, x, :], start=(x == 0), stop=(x == n - 1))
+            for x in range(PIECES):
+                nc.tensor.matmul(
+                    out=prep[:], lhsT=mean_w[:], rhs=pairs[b][:, x, :], start=(x == 0), stop=(x == PIECES - 1)
+                )
             preps[b] = prep
 
         def mean_copy(b):
@@ -102,20 +105,20 @@ def tile_scaleddotproductattention_kernel(tc, query_in, key_in, value_in, out):
             nc.vector.tensor_copy(out=mean[:], in_=preps[b][:])
             means[b] = mean
 
-        def v_regroup(b):
-            v_grp = opnd.tile([P, PASSES, D, PACK], BF16, align_bytes=64)
-            for g in range(PASSES):
-                for lo in range(0, D, D // 2):
-                    cols = slice(lo, lo + D // 2)
-                    nc.gpsimd.tensor_scalar(
-                        out=v_grp[:, g, cols, :],
-                        in0=v_raws[b][:, g, :, cols].rearrange("p t d -> p d t"),
-                        scalar1=1.0,
-                        scalar2=0.0,
-                        op0=ALU.mult,
-                        op1=ALU.add,
-                    )
-            v_grps[b] = v_grp
+        def v_regroup(b, x):
+            if x == 0:
+                v_grp = opnd.tile([P, PASSES, D, PACK], BF16, align_bytes=64)
+                v_grps[b] = v_grp
+            g, half = divmod(x, 2)
+            cols = slice(half * (D // 2), (half + 1) * (D // 2))
+            nc.gpsimd.tensor_scalar(
+                out=v_grps[b][:, g, cols, :],
+                in0=v_raws[b][:, g, :, cols].rearrange("p t d -> p d t"),
+                scalar1=1.0,
+                scalar2=0.0,
+                op0=ALU.mult,
+                op1=ALU.add,
+            )
 
         def v_quantise(b):
             v_code = opnd.tile([P, PASSES * D], U32, align_bytes=64)
@@ -173,13 +176,27 @@ def tile_scaleddotproductattention_kernel(tc, query_in, key_in, value_in, out):
                 nc.tensor.transpose(xt[:, c, :], e_tiles[n][:, c * P : (c + 1) * P], ident[:])
             x_tiles[n] = xt
 
-        def copy_out(n, on_vector):
-            grp = work.tile([P, PASSES, P, PACK], BF16, align_bytes=64)
-            src = x_tiles[n][:].rearrange("p (g t) q -> p g q t", g=PASSES)
-            if on_vector:
-                nc.vector.tensor_copy(out=grp[:], in_=src)
+        def copy_out(n):
+            if n % UNITS in GPSIMD_UNITS:
+                flat = work.tile([P, PASSES * PACK, P], BF16)
+                nc.scalar.copy(out=flat[:], in_=x_tiles[n][:])
+                flats[n] = flat
             else:
-                nc.scalar.copy(out=grp[:], in_=src)
+                grp = grouped.tile([P, PASSES, P, PACK], BF16, align_bytes=64)
+                nc.scalar.copy(out=grp[:], in_=x_tiles[n][:].rearrange("p (g t) q -> p g q t", g=PASSES))
+                grps[n] = grp
+
+        def e_regroup(n):
+            grp = grouped.tile([P, PASSES, P, PACK], BF16, align_bytes=64)
+            for g in range(PASSES):
+                nc.gpsimd.tensor_scalar(
+                    out=grp[:, g, :, :],
+                    in0=flats[n][:, g * PACK : (g + 1) * PACK, :].rearrange("p t q -> p q t"),
+                    scalar1=1.0,
+                    scalar2=0.0,
+                    op0=ALU.mult,
+                    op1=ALU.add,
+                )
             grps[n] = grp
 
         def e_quantise(n):
@@ -244,58 +261,63 @@ def tile_scaleddotproductattention_kernel(tc, query_in, key_in, value_in, out):
         q_copy(0)
         k_transposes(0, ps_x, "xt")
         k_copy(0)
-        pair_sums(0)
-        v_regroup(0)
+        for x in range(PIECES):
+            pair_sum(0, x)
+        for x in range(PIECES):
+            v_regroup(0, x)
 
-        for k in range(-1, N_UNITS + 7):
-            group = k // RING - 1
-            new_group = k % RING == 0 and 0 <= group < N_UNITS // RING
-            vector_copies = (k - 1) % UNITS in VECTOR_UNITS
+        for k in range(-1, N_UNITS + 8):
+            group = (k - 1) // RING - 1
+            new_group = (k - 1) % RING == 0 and 0 <= group < N_UNITS // RING
             if 0 <= k + 1 < N_UNITS:
                 scores(k + 1)
-            if 0 <= k - 3 < N_UNITS:
-                e_quantise(k - 3)
+            if 0 <= k - 4 < N_UNITS:
+                e_quantise(k - 4)
             if 0 <= k + 1 < N_UNITS:
                 row_max(k + 1)
             if new_group:
                 row_sums(group)
             if 0 <= k - 1 < N_UNITS:
                 e_transposes(k - 1)
-            if 0 <= k - 4 < N_UNITS:
-                pv_passes(k - 4)
-            if 0 <= k - 6 < N_UNITS:
-                finish(k - 6)
+            if 0 <= k - 5 < N_UNITS:
+                pv_passes(k - 5)
+            if 0 <= k - 7 < N_UNITS:
+                finish(k - 7)
             if 0 <= k + 1 < N_UNITS:
                 exp_bias(k + 1)
-            if 0 <= k - 1 < N_UNITS and vector_copies:
-                copy_out(k - 1, True)
             if new_group:
                 reciprocals(group)
             if 0 <= k < N_UNITS:
                 exps(k)
-            if 0 <= k - 1 < N_UNITS and not vector_copies:
-                copy_out(k - 1, False)
-            nb = k // UNITS + 1
-            phase = k % UNITS
+            if 0 <= k - 1 < N_UNITS:
+                copy_out(k - 1)
+            if 0 <= k - 2 < N_UNITS and (k - 2) % UNITS in GPSIMD_UNITS:
+                e_regroup(k - 2)
+            batch, phase = divmod(k, UNITS)
+            nb = batch + 1
             if k == -1:
                 mean_matmuls(0)
                 mean_copy(0)
                 v_quantise(0)
-            if k >= 0 and nb < B:
+            if 1 <= batch < B:
                 if phase == 0:
-                    if nb + 2 < B:
-                        load(nb + 2)
-                    q_transposes(nb)
-                    pair_sums(nb)
+                    mean_matmuls(batch)
                 elif phase == 1:
-                    q_copy(nb)
-                    v_regroup(nb)
+                    mean_copy(batch)
+            if k >= 0 and nb < B:
+                if phase < PIECES:
+                    v_regroup(nb, phase)
+                else:
+                    pair_sum(nb, phase - PIECES)
+                if phase == 0 and nb + 2 < B:
+                    load(nb + 2)
                 elif phase == 2:
-                    k_transposes(nb, ps_prep, "prep")
+                    q_transposes(nb)
                 elif phase == 3:
-                    k_copy(nb)
+                    q_copy(nb)
                 elif phase == 4:
-                    mean_matmuls(nb)
-                    v_quantise(nb)
+                    k_transposes(nb, ps_prep, "prep")
                 elif phase == 5:
-                    mean_copy(nb)
+                    k_copy(nb)
+                elif phase == 6:
+                    v_quantise(nb)

@@ -22,7 +22,7 @@ HALF = 512
 N_UNITS = B * UNITS
 RING = 4
 PIECES = 4
-GPSIMD_UNITS = (1, 4, 7)
+GPSIMD_UNITS = (1, 3, 5, 7)
 SCALE = 1.0 / math.sqrt(D)
 FLOPS = 4 * B * T * T * D
 

@@ -22,7 +22,7 @@ HALF = 512
 N_UNITS = B * UNITS
 RING = 4
 PIECES = 4
-GPSIMD_UNITS = (1, 3, 5, 7)
+WORDS = 2
 SCALE = 1.0 / math.sqrt(D)
 FLOPS = 4 * B * T * T * D
 
@@ -44,6 +44,8 @@ def tile_scaleddotproductattention_kernel(tc, query_in, key_in, value_in, out):
 
         ident = const.tile([P, P], BF16)
         masks.make_identity(nc, ident[:])
+        ident_w = const.tile([P, P], F32)
+        masks.make_identity(nc, ident_w[:])
         mean_w = const.tile([P, P], F32)
         nc.vector.memset(mean_w[:], 1.0 / T)
         pv = ps_pv.tile([P, RING, D], F32)
@@ -51,7 +53,7 @@ def tile_scaleddotproductattention_kernel(tc, query_in, key_in, value_in, out):
         q_raws, k_raws, v_raws = {}, {}, {}
         q_ts, k_ts, v_codes, v_scales, means, pairs, v_grps, preps = {}, {}, {}, {}, {}, {}, {}, {}
         s_tiles, biases, e_tiles, x_tiles, grps, e_codes, e_scales = {}, {}, {}, {}, {}, {}, {}
-        sums, totals, recips, results, maxes, flats = {}, {}, {}, {}, {}, {}
+        sums, totals, recips, results, maxes = {}, {}, {}, {}, {}
 
         def load(b):
             q_raw = raw.tile([P, UNITS, D], BF16)
@@ -82,7 +84,10 @@ def tile_scaleddotproductattention_kernel(tc, query_in, key_in, value_in, out):
 
         def k_copy(b):
             k_t = opnd.tile([P, T], BF16)
-            nc.vector.tensor_copy(out=k_t[:], in_=preps[b][:].rearrange("p c k -> p (c k)"))
+            nc.vector.tensor_copy(
+                out=k_t[:].rearrange("p (c k e) -> p c k e", c=PASSES * WORDS, e=2),
+                in_=preps[b][:].rearrange("p (c e) k -> p c k e", e=2),
+            )
             k_ts[b] = k_t
 
         def pair_sum(b, x):
@@ -171,32 +176,18 @@ def tile_scaleddotproductattention_kernel(tc, query_in, key_in, value_in, out):
             e_tiles[n] = e_sb
 
         def e_transposes(n):
-            xt = ps_x.tile([P, PASSES * PACK, P], BF16)
-            for c in range(PASSES * PACK):
-                nc.tensor.transpose(xt[:, c, :], e_tiles[n][:, c * P : (c + 1) * P], ident[:])
+            xt = ps_x.tile([P, PASSES * WORDS, P], F32)
+            words = e_tiles[n][:].bitcast(F32)
+            for c in range(PASSES * WORDS):
+                nc.tensor.transpose(xt[:, c, :], words[:, c * P : (c + 1) * P], ident_w[:])
             x_tiles[n] = xt
 
         def copy_out(n):
-            if n % UNITS in GPSIMD_UNITS:
-                flat = work.tile([P, PASSES * PACK, P], BF16)
-                nc.scalar.copy(out=flat[:], in_=x_tiles[n][:])
-                flats[n] = flat
-            else:
-                grp = grouped.tile([P, PASSES, P, PACK], BF16, align_bytes=64)
-                nc.scalar.copy(out=grp[:], in_=x_tiles[n][:].rearrange("p (g t) q -> p g q t", g=PASSES))
-                grps[n] = grp
-
-        def e_regroup(n):
-            grp = grouped.tile([P, PASSES, P, PACK], BF16, align_bytes=64)
-            for g in range(PASSES):
-                nc.gpsimd.tensor_scalar(
-                    out=grp[:, g, :, :],
-                    in0=flats[n][:, g * PACK : (g + 1) * PACK, :].rearrange("p t q -> p q t"),
-                    scalar1=1.0,
-                    scalar2=0.0,
-                    op0=ALU.mult,
-                    op1=ALU.add,
-                )
+            grp = grouped.tile([P, PASSES * P * PACK], BF16, align_bytes=64)
+            nc.scalar.copy(
+                out=grp[:].bitcast(F32).rearrange("p (g q u) -> p g q u", g=PASSES, u=WORDS),
+                in_=x_tiles[n][:].rearrange("p (g u) q -> p g q u", g=PASSES),
+            )
             grps[n] = grp
 
         def e_quantise(n):
@@ -205,7 +196,7 @@ def tile_scaleddotproductattention_kernel(tc, query_in, key_in, value_in, out):
             nc.vector.quantize_mx(
                 out=e_code[:].bitcast(FP8X4),
                 scales=e_scale[:],
-                in_=grps[n][:].rearrange("p g q t -> p (g q t)"),
+                in_=grps[n][:],
             )
             e_codes[n], e_scales[n] = e_code, e_scale
 
@@ -291,8 +282,6 @@ def tile_scaleddotproductattention_kernel(tc, query_in, key_in, value_in, out):
                 exps(k)
             if 0 <= k - 1 < N_UNITS:
                 copy_out(k - 1)
-            if 0 <= k - 2 < N_UNITS and (k - 2) % UNITS in GPSIMD_UNITS:
-                e_regroup(k - 2)
             batch, phase = divmod(k, UNITS)
             nb = batch + 1
             if k == -1:

@@ -72,7 +72,7 @@ def tile_scaleddotproductattention_kernel(tc, query_in, key_in, value_in, out):
 
         def q_copy(b):
             q_t = opnd.tile([P, UNITS, P], BF16)
-            nc.vector.tensor_copy(out=q_t[:], in_=preps[b][:])
+            nc.scalar.copy(out=q_t[:], in_=preps[b][:])
             q_ts[b] = q_t
 
         def k_transposes(b, pool, tag):
@@ -84,7 +84,7 @@ def tile_scaleddotproductattention_kernel(tc, query_in, key_in, value_in, out):
 
         def k_copy(b):
             k_t = opnd.tile([P, T], BF16)
-            nc.vector.tensor_copy(
+            nc.scalar.copy(
                 out=k_t[:].rearrange("p (c k e) -> p c k e", c=PASSES * WORDS, e=2),
                 in_=preps[b][:].rearrange("p (c e) k -> p c k e", e=2),
             )
@@ -107,7 +107,7 @@ def tile_scaleddotproductattention_kernel(tc, query_in, key_in, value_in, out):
 
         def mean_copy(b):
             mean = opnd.tile([P, D], F32)
-            nc.vector.tensor_copy(out=mean[:], in_=preps[b][:])
+            nc.scalar.copy(out=mean[:], in_=preps[b][:])
             means[b] = mean
 
         def v_regroup(b, x):

@@ -37,10 +37,9 @@ def tile_scaleddotproductattention_kernel(tc, query_in, key_in, value_in, out):
         grouped = ctx.enter_context(tc.tile_pool(name="grouped", bufs=5))
         small = ctx.enter_context(tc.tile_pool(name="small", bufs=4))
         outp = ctx.enter_context(tc.tile_pool(name="outp", bufs=2))
-        ps_s = ctx.enter_context(tc.psum_pool(name="ps_s", bufs=4))
+        ps_s = ctx.enter_context(tc.psum_pool(name="ps_s", bufs=5))
         ps_x = ctx.enter_context(tc.psum_pool(name="ps_x", bufs=2))
         ps_pv = ctx.enter_context(tc.psum_pool(name="ps_pv", bufs=1))
-        ps_prep = ctx.enter_context(tc.psum_pool(name="ps_prep", bufs=1))
 
         ident = const.tile([P, P], BF16)
         masks.make_identity(nc, ident[:])
@@ -65,7 +64,7 @@ def tile_scaleddotproductattention_kernel(tc, query_in, key_in, value_in, out):
             q_raws[b], k_raws[b], v_raws[b] = q_raw, k_raw, v_raw
 
         def q_transposes(b):
-            prep = ps_prep.tile([P, UNITS, P], BF16, tag="prep")
+            prep = ps_x.tile([P, UNITS, P], BF16, tag="xt")
             for i in range(UNITS):
                 nc.tensor.transpose(prep[:, i, :], q_raws[b][:, i, :], ident[:])
             preps[b] = prep
@@ -75,8 +74,8 @@ def tile_scaleddotproductattention_kernel(tc, query_in, key_in, value_in, out):
             nc.scalar.copy(out=q_t[:], in_=preps[b][:])
             q_ts[b] = q_t
 
-        def k_transposes(b, pool, tag):
-            prep = pool.tile([P, PASSES * PACK, P], BF16, tag=tag)
+        def k_transposes(b):
+            prep = ps_x.tile([P, PASSES * PACK, P], BF16, tag="xt")
             for g in range(PASSES):
                 for t in range(PACK):
                     nc.tensor.transpose(prep[:, g * PACK + t, :], k_raws[b][:, g, t, :], ident[:])
@@ -98,7 +97,7 @@ def tile_scaleddotproductattention_kernel(tc, query_in, key_in, value_in, out):
             nc.gpsimd.tensor_tensor(out=pairs[b][:, x, :], in0=halves[:, x, 0, :], in1=halves[:, x, 1, :], op=ALU.add)
 
         def mean_matmuls(b):
-            prep = ps_prep.tile([P, D], F32, tag="prep")
+            prep = ps_x.tile([P, D], F32, tag="xt")
             for x in range(PIECES):
                 nc.tensor.matmul(
                     out=prep[:], lhsT=mean_w[:], rhs=pairs[b][:, x, :], start=(x == 0), stop=(x == PIECES - 1)
@@ -250,7 +249,7 @@ def tile_scaleddotproductattention_kernel(tc, query_in, key_in, value_in, out):
             load(b)
         q_transposes(0)
         q_copy(0)
-        k_transposes(0, ps_x, "xt")
+        k_transposes(0)
         k_copy(0)
         for x in range(PIECES):
             pair_sum(0, x)
@@ -278,21 +277,25 @@ def tile_scaleddotproductattention_kernel(tc, query_in, key_in, value_in, out):
                 exp_bias(k + 1)
             if new_group:
                 reciprocals(group)
-            if 0 <= k < N_UNITS:
-                exps(k)
-            if 0 <= k - 1 < N_UNITS:
-                copy_out(k - 1)
             batch, phase = divmod(k, UNITS)
             nb = batch + 1
+            if 0 <= k < N_UNITS:
+                exps(k)
+            if 1 <= batch < B and phase == 1:
+                mean_copy(batch)
+            if k >= 0 and nb < B:
+                if phase == 3:
+                    q_copy(nb)
+                elif phase == 5:
+                    k_copy(nb)
+            if 0 <= k - 1 < N_UNITS:
+                copy_out(k - 1)
             if k == -1:
                 mean_matmuls(0)
                 mean_copy(0)
                 v_quantise(0)
-            if 1 <= batch < B:
-                if phase == 0:
-                    mean_matmuls(batch)
-                elif phase == 1:
-                    mean_copy(batch)
+            if 1 <= batch < B and phase == 0:
+                mean_matmuls(batch)
             if k >= 0 and nb < B:
                 if phase < PIECES:
                     v_regroup(nb, phase)
@@ -302,11 +305,7 @@ def tile_scaleddotproductattention_kernel(tc, query_in, key_in, value_in, out):
                     load(nb + 2)
                 elif phase == 2:
                     q_transposes(nb)
-                elif phase == 3:
-                    q_copy(nb)
                 elif phase == 4:
-                    k_transposes(nb, ps_prep, "prep")
-                elif phase == 5:
-                    k_copy(nb)
+                    k_transposes(nb)
                 elif phase == 6:
                     v_quantise(nb)

@@ -34,7 +34,7 @@ def tile_scaleddotproductattention_kernel(tc, query_in, key_in, value_in, out):
         raw = ctx.enter_context(tc.tile_pool(name="raw", bufs=3))
         opnd = ctx.enter_context(tc.tile_pool(name="opnd", bufs=3))
         work = ctx.enter_context(tc.tile_pool(name="work", bufs=3))
-        grouped = ctx.enter_context(tc.tile_pool(name="grouped", bufs=5))
+        grouped = ctx.enter_context(tc.tile_pool(name="grouped", bufs=3))
         small = ctx.enter_context(tc.tile_pool(name="small", bufs=4))
         outp = ctx.enter_context(tc.tile_pool(name="outp", bufs=2))
         ps_s = ctx.enter_context(tc.psum_pool(name="ps_s", bufs=5))
@@ -57,8 +57,11 @@ def tile_scaleddotproductattention_kernel(tc, query_in, key_in, value_in, out):
         def load(b):
             q_raw = raw.tile([P, UNITS, D], BF16)
             nc.sync.dma_start(out=q_raw[:], in_=query_in[b].rearrange("(p i) d -> p i d", i=UNITS))
-            k_raw = raw.tile([P, PASSES, PACK, D], BF16)
-            nc.sync.dma_start(out=k_raw[:], in_=key_in[b].rearrange("(g p t) d -> p g t d", g=PASSES, t=PACK))
+            k_raw = raw.tile([P, 2 * PASSES, WORDS, D], BF16)
+            k_rows = key_in[b].rearrange("(c a u e) d -> e a c u d", c=2 * PASSES, u=WORDS, e=2)
+            for e in range(2):
+                for u in range(WORDS):
+                    nc.sync.dma_start(out=k_raw[e:P:2, :, u, :], in_=k_rows[e, :, :, u, :])
             v_raw = raw.tile([P, PASSES, PACK, D], BF16)
             nc.sync.dma_start(out=v_raw[:], in_=value_in[b].rearrange("(g p t) d -> p g t d", g=PASSES, t=PACK))
             q_raws[b], k_raws[b], v_raws[b] = q_raw, k_raw, v_raw
@@ -71,22 +74,22 @@ def tile_scaleddotproductattention_kernel(tc, query_in, key_in, value_in, out):
 
         def q_copy(b):
             q_t = opnd.tile([P, UNITS, P], BF16)
-            nc.scalar.copy(out=q_t[:], in_=preps[b][:])
+            nc.vector.tensor_copy(out=q_t[:], in_=preps[b][:])
             q_ts[b] = q_t
 
         def k_transposes(b):
             prep = ps_x.tile([P, PASSES * PACK, P], BF16, tag="xt")
             for g in range(PASSES):
-                for t in range(PACK):
-                    nc.tensor.transpose(prep[:, g * PACK + t, :], k_raws[b][:, g, t, :], ident[:])
+                for u in range(WORDS):
+                    for half in range(2):
+                        nc.tensor.transpose(
+                            prep[:, g * PACK + u * 2 + half, :], k_raws[b][:, g * 2 + half, u, :], ident[:]
+                        )
             preps[b] = prep
 
         def k_copy(b):
             k_t = opnd.tile([P, T], BF16)
-            nc.scalar.copy(
-                out=k_t[:].rearrange("p (c k e) -> p c k e", c=PASSES * WORDS, e=2),
-                in_=preps[b][:].rearrange("p (c e) k -> p c k e", e=2),
-            )
+            nc.scalar.copy(out=k_t[:], in_=preps[b][:].rearrange("p c k -> p (c k)"))
             k_ts[b] = k_t
 
         def pair_sum(b, x):
@@ -182,32 +185,36 @@ def tile_scaleddotproductattention_kernel(tc, query_in, key_in, value_in, out):
             x_tiles[n] = xt
 
         def copy_out(n):
-            grp = grouped.tile([P, PASSES * P * PACK], BF16, align_bytes=64)
+            if n % 2 == 0:
+                grp = grouped.tile([P, 2 * T], BF16, align_bytes=64)
+                grps[n // 2] = grp
             nc.scalar.copy(
-                out=grp[:].bitcast(F32).rearrange("p (g q u) -> p g q u", g=PASSES, u=WORDS),
+                out=grps[n // 2][:, (n % 2) * T : (n % 2 + 1) * T]
+                .bitcast(F32)
+                .rearrange("p (g q u) -> p g q u", g=PASSES, u=WORDS),
                 in_=x_tiles[n][:].rearrange("p (g u) q -> p g q u", g=PASSES),
             )
-            grps[n] = grp
 
-        def e_quantise(n):
-            e_code = work.tile([P, PASSES * P], U32, align_bytes=64)
-            e_scale = work.tile([P, PASSES * P], U8, align_bytes=64)
+        def e_quantise(pair):
+            e_code = work.tile([P, 2 * PASSES * P], U32, align_bytes=64)
+            e_scale = work.tile([P, 2 * PASSES * P], U8, align_bytes=64)
             nc.vector.quantize_mx(
                 out=e_code[:].bitcast(FP8X4),
                 scales=e_scale[:],
-                in_=grps[n][:],
+                in_=grps[pair][:],
             )
-            e_codes[n], e_scales[n] = e_code, e_scale
+            e_codes[pair], e_scales[pair] = e_code, e_scale
 
         def pv_passes(n):
             b = n // UNITS
             slot = n % RING
             for g in range(PASSES):
                 cols = slice(g * P, (g + 1) * P)
+                e_cols = slice((n % 2 * PASSES + g) * P, (n % 2 * PASSES + g + 1) * P)
                 nc.tensor.matmul_mx(
                     out=pv[:, slot, :],
-                    lhsT=e_codes[n][:, cols].bitcast(FP8X4),
-                    lhsT_scale=e_scales[n][:, cols],
+                    lhsT=e_codes[n // 2][:, e_cols].bitcast(FP8X4),
+                    lhsT_scale=e_scales[n // 2][:, e_cols],
                     rhs=v_codes[b][:, cols].bitcast(FP8X4),
                     rhs_scale=v_scales[b][:, cols],
                     start=(g == 0),
@@ -216,7 +223,7 @@ def tile_scaleddotproductattention_kernel(tc, query_in, key_in, value_in, out):
 
         def row_sums(j):
             total = small.tile([P, RING], F32)
-            nc.vector.tensor_reduce(out=total[:], in_=sums[j][:], axis=AX.X, op=ALU.add)
+            nc.gpsimd.tensor_tensor(out=total[:], in0=sums[j][:, :, 0], in1=sums[j][:, :, 1], op=ALU.add)
             totals[j] = total
 
         def reciprocals(j):
@@ -259,18 +266,21 @@ def tile_scaleddotproductattention_kernel(tc, query_in, key_in, value_in, out):
         for k in range(-1, N_UNITS + 8):
             group = (k - 1) // RING - 1
             new_group = (k - 1) % RING == 0 and 0 <= group < N_UNITS // RING
+            if k >= 0 and k // UNITS + 1 < B and k % UNITS == 3:
+                q_copy(k // UNITS + 1)
             if 0 <= k + 1 < N_UNITS:
                 scores(k + 1)
-            if 0 <= k - 4 < N_UNITS:
-                e_quantise(k - 4)
+            if 0 <= k - 3 < N_UNITS and (k - 3) % 2 == 1:
+                e_quantise((k - 3) // 2)
             if 0 <= k + 1 < N_UNITS:
                 row_max(k + 1)
             if new_group:
                 row_sums(group)
             if 0 <= k - 1 < N_UNITS:
                 e_transposes(k - 1)
-            if 0 <= k - 5 < N_UNITS:
+            if 0 <= k - 4 < N_UNITS and (k - 4) % 2 == 1:
                 pv_passes(k - 5)
+                pv_passes(k - 4)
             if 0 <= k - 7 < N_UNITS:
                 finish(k - 7)
             if 0 <= k + 1 < N_UNITS:
@@ -283,11 +293,8 @@ def tile_scaleddotproductattention_kernel(tc, query_in, key_in, value_in, out):
                 exps(k)
             if 1 <= batch < B and phase == 1:
                 mean_copy(batch)
-            if k >= 0 and nb < B:
-                if phase == 3:
-                    q_copy(nb)
-                elif phase == 5:
-                    k_copy(nb)
+            if k >= 0 and nb < B and phase == 5:
+                k_copy(nb)
             if 0 <= k - 1 < N_UNITS:
                 copy_out(k - 1)
             if k == -1:

@@ -266,10 +266,22 @@ def tile_scaleddotproductattention_kernel(tc, query_in, key_in, value_in, out):
         for k in range(-1, N_UNITS + 8):
             group = (k - 1) // RING - 1
             new_group = (k - 1) % RING == 0 and 0 <= group < N_UNITS // RING
-            if k >= 0 and k // UNITS + 1 < B and k % UNITS == 3:
-                q_copy(k // UNITS + 1)
+            batch, phase = divmod(k, UNITS)
+            nb = batch + 1
+            prepare = k >= 0 and nb < B
+            if prepare and phase == 3:
+                q_copy(nb)
             if 0 <= k + 1 < N_UNITS:
                 scores(k + 1)
+            if 1 <= batch < B and phase == 0:
+                mean_matmuls(batch)
+            if prepare and phase == 2:
+                q_transposes(nb)
+            if prepare and phase == 4:
+                k_transposes(nb)
+            if 0 <= k - 4 < N_UNITS and (k - 4) % 2 == 1:
+                pv_passes(k - 5)
+                pv_passes(k - 4)
             if 0 <= k - 3 < N_UNITS and (k - 3) % 2 == 1:
                 e_quantise((k - 3) // 2)
             if 0 <= k + 1 < N_UNITS:
@@ -278,22 +290,17 @@ def tile_scaleddotproductattention_kernel(tc, query_in, key_in, value_in, out):
                 row_sums(group)
             if 0 <= k - 1 < N_UNITS:
                 e_transposes(k - 1)
-            if 0 <= k - 4 < N_UNITS and (k - 4) % 2 == 1:
-                pv_passes(k - 5)
-                pv_passes(k - 4)
             if 0 <= k - 7 < N_UNITS:
                 finish(k - 7)
             if 0 <= k + 1 < N_UNITS:
                 exp_bias(k + 1)
             if new_group:
                 reciprocals(group)
-            batch, phase = divmod(k, UNITS)
-            nb = batch + 1
             if 0 <= k < N_UNITS:
                 exps(k)
-            if 1 <= batch < B and phase == 1:
+            if 1 <= batch < B and phase == 0:
                 mean_copy(batch)
-            if k >= 0 and nb < B and phase == 5:
+            if prepare and phase == 4:
                 k_copy(nb)
             if 0 <= k - 1 < N_UNITS:
                 copy_out(k - 1)
@@ -301,18 +308,12 @@ def tile_scaleddotproductattention_kernel(tc, query_in, key_in, value_in, out):
                 mean_matmuls(0)
                 mean_copy(0)
                 v_quantise(0)
-            if 1 <= batch < B and phase == 0:
-                mean_matmuls(batch)
-            if k >= 0 and nb < B:
+            if prepare:
                 if phase < PIECES:
                     v_regroup(nb, phase)
                 else:
                     pair_sum(nb, phase - PIECES)
                 if phase == 0 and nb + 2 < B:
                     load(nb + 2)
-                elif phase == 2:
-                    q_transposes(nb)
-                elif phase == 4:
-                    k_transposes(nb)
-                elif phase == 6:
+                if phase == 7:
                     v_quantise(nb)

@@ -22,6 +22,7 @@ HALF = 512
 N_UNITS = B * UNITS
 RING = 4
 PIECES = 4
+WARM_UP = 4
 WORDS = 2
 SCALE = 1.0 / math.sqrt(D)
 FLOPS = 4 * B * T * T * D
@@ -48,6 +49,8 @@ def tile_scaleddotproductattention_kernel(tc, query_in, key_in, value_in, out):
         mean_w = const.tile([P, P], F32)
         nc.vector.memset(mean_w[:], 1.0 / T)
         pv = ps_pv.tile([P, RING, D], F32)
+        idle_rhs = const.tile([P, HALF], BF16)
+        nc.vector.memset(idle_rhs[:], 0.0)
 
         q_raws, k_raws, v_raws = {}, {}, {}
         q_ts, k_ts, v_codes, v_scales, means, pairs, v_grps, preps = {}, {}, {}, {}, {}, {}, {}, {}
@@ -55,13 +58,13 @@ def tile_scaleddotproductattention_kernel(tc, query_in, key_in, value_in, out):
         sums, totals, recips, results, maxes = {}, {}, {}, {}, {}
 
         def load(b):
-            q_raw = raw.tile([P, UNITS, D], BF16)
-            nc.sync.dma_start(out=q_raw[:], in_=query_in[b].rearrange("(p i) d -> p i d", i=UNITS))
             k_raw = raw.tile([P, 2 * PASSES, WORDS, D], BF16)
             k_rows = key_in[b].rearrange("(c a u e) d -> e a c u d", c=2 * PASSES, u=WORDS, e=2)
             for e in range(2):
                 for u in range(WORDS):
                     nc.sync.dma_start(out=k_raw[e:P:2, :, u, :], in_=k_rows[e, :, :, u, :])
+            q_raw = raw.tile([P, UNITS, D], BF16)
+            nc.sync.dma_start(out=q_raw[:], in_=query_in[b].rearrange("(p i) d -> p i d", i=UNITS))
             v_raw = raw.tile([P, PASSES, PACK, D], BF16)
             nc.sync.dma_start(out=v_raw[:], in_=value_in[b].rearrange("(g p t) d -> p g t d", g=PASSES, t=PACK))
             q_raws[b], k_raws[b], v_raws[b] = q_raw, k_raw, v_raw
@@ -245,8 +248,8 @@ def tile_scaleddotproductattention_kernel(tc, query_in, key_in, value_in, out):
                 op0=ALU.mult,
                 op1=ALU.subtract,
             )
-            if slot == RING - 1:
-                rows = slice(i - RING + 1, i + 1)
+            if slot % 2 == 1:
+                rows = slice(i - 1, i + 1)
                 nc.sync.dma_start(
                     out=out[b].rearrange("(p i) d -> p i d", i=UNITS)[:, rows, :], in_=results[b][:, rows, :]
                 )
@@ -254,10 +257,13 @@ def tile_scaleddotproductattention_kernel(tc, query_in, key_in, value_in, out):
         ctx.enter_context(tc.manual_schedule())
         for b in range(3):
             load(b)
-        q_transposes(0)
-        q_copy(0)
+        for w in range(WARM_UP):
+            idle_ps = ps_s.tile([P, HALF], F32, tag="s_ps")
+            nc.tensor.matmul(out=idle_ps[:], lhsT=ident[:], rhs=idle_rhs[:], start=True, stop=True)
         k_transposes(0)
         k_copy(0)
+        q_transposes(0)
+        q_copy(0)
         for x in range(PIECES):
             pair_sum(0, x)
         for x in range(PIECES):
@@ -304,7 +310,7 @@ def tile_scaleddotproductattention_kernel(tc, query_in, key_in, value_in, out):
                 k_copy(nb)
             if 0 <= k - 1 < N_UNITS:
                 copy_out(k - 1)
-            if k == -1:
+            if k == 1:
                 mean_matmuls(0)
                 mean_copy(0)
                 v_quantise(0)

@@ -288,16 +288,17 @@ def tile_scaleddotproductattention_kernel(tc, query_in, key_in, value_in, out):
             if 0 <= k - 4 < N_UNITS and (k - 4) % 2 == 1:
                 pv_passes(k - 5)
                 pv_passes(k - 4)
-            if 0 <= k - 3 < N_UNITS and (k - 3) % 2 == 1:
-                e_quantise((k - 3) // 2)
             if 0 <= k + 1 < N_UNITS:
                 row_max(k + 1)
+            if 0 <= k - 3 < N_UNITS and (k - 3) % 2 == 1:
+                e_quantise((k - 3) // 2)
             if new_group:
                 row_sums(group)
             if 0 <= k - 1 < N_UNITS:
                 e_transposes(k - 1)
-            if 0 <= k - 7 < N_UNITS:
+            if 0 <= k - 7 < N_UNITS and k % 2 == 1:
                 finish(k - 7)
+                finish(k - 6)
             if 0 <= k + 1 < N_UNITS:
                 exp_bias(k + 1)
             if new_group:

@@ -24,6 +24,7 @@ RING = 4
 PIECES = 4
 WARM_UP = 4
 WORDS = 2
+VECTOR_HALVES = (0,)
 SCALE = 1.0 / math.sqrt(D)
 FLOPS = 4 * B * T * T * D
 
@@ -38,8 +39,8 @@ def tile_scaleddotproductattention_kernel(tc, query_in, key_in, value_in, out):
         grouped = ctx.enter_context(tc.tile_pool(name="grouped", bufs=3))
         small = ctx.enter_context(tc.tile_pool(name="small", bufs=4))
         outp = ctx.enter_context(tc.tile_pool(name="outp", bufs=2))
-        ps_s = ctx.enter_context(tc.psum_pool(name="ps_s", bufs=5))
-        ps_x = ctx.enter_context(tc.psum_pool(name="ps_x", bufs=2))
+        ps_s = ctx.enter_context(tc.psum_pool(name="ps_s", bufs=6))
+        ps_x = ctx.enter_context(tc.psum_pool(name="ps_x", bufs=1))
         ps_pv = ctx.enter_context(tc.psum_pool(name="ps_pv", bufs=1))
 
         ident = const.tile([P, P], BF16)
@@ -48,7 +49,10 @@ def tile_scaleddotproductattention_kernel(tc, query_in, key_in, value_in, out):
         masks.make_identity(nc, ident_w[:])
         mean_w = const.tile([P, P], F32)
         nc.vector.memset(mean_w[:], 1.0 / T)
-        pv = ps_pv.tile([P, RING, D], F32)
+        bank = ps_pv.tile([P, 4, D], F32)
+        pv = bank[:, 0:2, :]
+        spare = bank[:, 2:4, :].rearrange("p s d -> p (s d)")
+        spare_16 = spare.bitcast(BF16)
         idle_rhs = const.tile([P, HALF], BF16)
         nc.vector.memset(idle_rhs[:], 0.0)
 
@@ -69,31 +73,31 @@ def tile_scaleddotproductattention_kernel(tc, query_in, key_in, value_in, out):
             nc.sync.dma_start(out=v_raw[:], in_=value_in[b].rearrange("(g p t) d -> p g t d", g=PASSES, t=PACK))
             q_raws[b], k_raws[b], v_raws[b] = q_raw, k_raw, v_raw
 
-        def q_transposes(b):
-            prep = ps_x.tile([P, UNITS, P], BF16, tag="xt")
-            for i in range(UNITS):
-                nc.tensor.transpose(prep[:, i, :], q_raws[b][:, i, :], ident[:])
-            preps[b] = prep
+        def q_transposes(b, half, place):
+            for i in range(4):
+                nc.tensor.transpose(place[:, i * P : (i + 1) * P], q_raws[b][:, half * 4 + i, :], ident[:])
 
-        def q_copy(b):
-            q_t = opnd.tile([P, UNITS, P], BF16)
-            nc.vector.tensor_copy(out=q_t[:], in_=preps[b][:])
-            q_ts[b] = q_t
+        def q_copy(b, half):
+            if half == 0:
+                q_t = opnd.tile([P, T], BF16)
+                q_ts[b] = q_t
+            nc.vector.tensor_copy(out=q_ts[b][:, half * HALF : (half + 1) * HALF], in_=spare_16)
 
-        def k_transposes(b):
-            prep = ps_x.tile([P, PASSES * PACK, P], BF16, tag="xt")
-            for g in range(PASSES):
-                for u in range(WORDS):
-                    for half in range(2):
-                        nc.tensor.transpose(
-                            prep[:, g * PACK + u * 2 + half, :], k_raws[b][:, g * 2 + half, u, :], ident[:]
-                        )
-            preps[b] = prep
+        def k_transposes(b, g, place):
+            for u in range(WORDS):
+                for e in range(2):
+                    c = u * 2 + e
+                    nc.tensor.transpose(place[:, c * P : (c + 1) * P], k_raws[b][:, g * 2 + e, u, :], ident[:])
 
-        def k_copy(b):
-            k_t = opnd.tile([P, T], BF16)
-            nc.scalar.copy(out=k_t[:], in_=preps[b][:].rearrange("p c k -> p (c k)"))
-            k_ts[b] = k_t
+        def k_copy(b, g):
+            if g == 0:
+                k_t = opnd.tile([P, T], BF16)
+                k_ts[b] = k_t
+            out_cols = k_ts[b][:, g * HALF : (g + 1) * HALF]
+            if g in VECTOR_HALVES:
+                nc.vector.tensor_copy(out=out_cols, in_=spare_16)
+            else:
+                nc.scalar.copy(out=out_cols, in_=spare_16)
 
         def pair_sum(b, x):
             if x == 0:
@@ -102,17 +106,15 @@ def tile_scaleddotproductattention_kernel(tc, query_in, key_in, value_in, out):
             halves = v_raws[b][:].rearrange("p g (u e) d -> p (g u) e d", e=2)
             nc.gpsimd.tensor_tensor(out=pairs[b][:, x, :], in0=halves[:, x, 0, :], in1=halves[:, x, 1, :], op=ALU.add)
 
-        def mean_matmuls(b):
-            prep = ps_x.tile([P, D], F32, tag="xt")
-            for x in range(PIECES):
-                nc.tensor.matmul(
-                    out=prep[:], lhsT=mean_w[:], rhs=pairs[b][:, x, :], start=(x == 0), stop=(x == PIECES - 1)
-                )
-            preps[b] = prep
+        def piece_sum(b, x, y):
+            nc.gpsimd.tensor_tensor(out=pairs[b][:, x, :], in0=pairs[b][:, x, :], in1=pairs[b][:, y, :], op=ALU.add)
+
+        def mean_matmul(b):
+            nc.tensor.matmul(out=spare[:, 0:D], lhsT=mean_w[:], rhs=pairs[b][:, 0, :], start=True, stop=True)
 
         def mean_copy(b):
             mean = opnd.tile([P, D], F32)
-            nc.scalar.copy(out=mean[:], in_=preps[b][:])
+            nc.vector.tensor_copy(out=mean[:], in_=spare[:, 0:D])
             means[b] = mean
 
         def v_regroup(b, x):
@@ -145,40 +147,41 @@ def tile_scaleddotproductattention_kernel(tc, query_in, key_in, value_in, out):
             for h in range(2):
                 s_ps = ps_s.tile([P, HALF], F32)
                 nc.tensor.matmul(
-                    out=s_ps[:], lhsT=q_ts[b][:, i, :], rhs=k_ts[b][:, h * HALF : (h + 1) * HALF], start=True, stop=True
+                    out=s_ps[:], lhsT=q_ts[b][:, i * P : (i + 1) * P], rhs=k_ts[b][:, h * HALF : (h + 1) * HALF], start=True, stop=True
                 )
                 s_tiles[(n, h)] = s_ps
 
-        def row_max(n):
-            mx = small.tile([P, 2], F32)
-            for h in range(2):
-                nc.vector.tensor_reduce(out=mx[:, h : h + 1], in_=s_tiles[(n, h)][:], axis=AX.X, op=ALU.max)
-            maxes[n] = mx
+        def row_max(n, h):
+            if h == 0:
+                mx = small.tile([P, 2], F32)
+                maxes[n] = mx
+            nc.vector.tensor_reduce(out=maxes[n][:, h : h + 1], in_=s_tiles[(n, h)][:], axis=AX.X, op=ALU.max)
 
         def exp_bias(n):
             mx = maxes[n]
             bias = small.tile([P, 1], F32)
-            nc.vector.tensor_scalar(
+            (nc.vector if n < 2 else nc.gpsimd).tensor_scalar(
                 out=bias[:], in0=mx[:, 0:1], scalar1=mx[:, 1:2], scalar2=-SCALE, op0=ALU.max, op1=ALU.mult
             )
             biases[n] = bias
 
-        def exps(n):
+        def exps(n, halves=(0, 1)):
             j, slot = divmod(n, RING)
-            if slot == 0:
+            if slot == 0 and 0 in halves:
                 rs = small.tile([P, RING, 2], F32)
                 sums[j] = rs
-            e_sb = work.tile([P, T], BF16)
-            for h in range(2):
+            if 0 in halves:
+                e_sb = work.tile([P, T], BF16)
+                e_tiles[n] = e_sb
+            for h in halves:
                 nc.scalar.activation(
-                    out=e_sb[:, h * HALF : (h + 1) * HALF],
+                    out=e_tiles[n][:, h * HALF : (h + 1) * HALF],
                     in_=s_tiles[(n, h)][:],
                     func=ACT.Exp,
                     bias=biases[n][:],
                     scale=SCALE,
                     accum_out=sums[j][:, slot, h : h + 1],
                 )
-            e_tiles[n] = e_sb
 
         def e_transposes(n):
             xt = ps_x.tile([P, PASSES * WORDS, P], F32)
@@ -187,11 +190,31 @@ def tile_scaleddotproductattention_kernel(tc, query_in, key_in, value_in, out):
                 nc.tensor.transpose(xt[:, c, :], words[:, c * P : (c + 1) * P], ident_w[:])
             x_tiles[n] = xt
 
+        def last_transposes(n, g):
+            xh = ps_s.tile([P, WORDS, P], F32, tag="s_ps")
+            words = e_tiles[n][:].bitcast(F32)
+            for u in range(WORDS):
+                c = g * WORDS + u
+                nc.tensor.transpose(xh[:, u, :], words[:, c * P : (c + 1) * P], ident_w[:])
+            x_tiles[(n, g)] = xh
+
+        def last_copy(n, g):
+            lo = (n % 2) * T + g * HALF
+            out_words = grps[n // 2][:, lo : lo + HALF].bitcast(F32).rearrange("p (q u) -> p q u", u=WORDS)
+            (nc.vector.tensor_copy if g == 0 else nc.scalar.copy)(out=out_words, in_=x_tiles[(n, g)][:].rearrange("p u q -> p q u"))
+
+        def last_quantise(n, lo, hi):
+            nc.vector.quantize_mx(
+                out=e_codes[n // 2][:, lo:hi].bitcast(FP8X4),
+                scales=e_scales[n // 2][:, lo:hi],
+                in_=grps[n // 2][:, PACK * lo : PACK * hi],
+            )
+
         def copy_out(n):
             if n % 2 == 0:
                 grp = grouped.tile([P, 2 * T], BF16, align_bytes=64)
                 grps[n // 2] = grp
-            nc.scalar.copy(
+            (nc.vector.tensor_copy if n == N_UNITS - 2 else nc.scalar.copy)(
                 out=grps[n // 2][:, (n % 2) * T : (n % 2 + 1) * T]
                 .bitcast(F32)
                 .rearrange("p (g q u) -> p g q u", g=PASSES, u=WORDS),
@@ -210,7 +233,7 @@ def tile_scaleddotproductattention_kernel(tc, query_in, key_in, value_in, out):
 
         def pv_passes(n):
             b = n // UNITS
-            slot = n % RING
+            slot = n % 2
             for g in range(PASSES):
                 cols = slice(g * P, (g + 1) * P)
                 e_cols = slice((n % 2 * PASSES + g) * P, (n % 2 * PASSES + g + 1) * P)
@@ -242,14 +265,14 @@ def tile_scaleddotproductattention_kernel(tc, query_in, key_in, value_in, out):
                 results[b] = res
             nc.vector.scalar_tensor_tensor(
                 out=results[b][:, i, :],
-                in0=pv[:, slot, :],
+                in0=pv[:, n % 2, :],
                 scalar=recips[j][:, slot : slot + 1],
                 in1=means[b][:],
                 op0=ALU.mult,
                 op1=ALU.subtract,
             )
-            if slot % 2 == 1:
-                rows = slice(i - 1, i + 1)
+            if n % 2 == 1 or n >= N_UNITS - 2:
+                rows = slice(i - 1 if n < N_UNITS - 2 else i, i + 1)
                 nc.sync.dma_start(
                     out=out[b].rearrange("(p i) d -> p i d", i=UNITS)[:, rows, :], in_=results[b][:, rows, :]
                 )
@@ -260,61 +283,76 @@ def tile_scaleddotproductattention_kernel(tc, query_in, key_in, value_in, out):
         for w in range(WARM_UP):
             idle_ps = ps_s.tile([P, HALF], F32, tag="s_ps")
             nc.tensor.matmul(out=idle_ps[:], lhsT=ident[:], rhs=idle_rhs[:], start=True, stop=True)
-        k_transposes(0)
-        k_copy(0)
-        q_transposes(0)
-        q_copy(0)
-        for x in range(PIECES):
-            pair_sum(0, x)
-        for x in range(PIECES):
-            v_regroup(0, x)
+        k_t = opnd.tile([P, T], BF16)
+        q_t = opnd.tile([P, T], BF16)
+        k_ts[0], q_ts[0] = k_t, q_t
+        for g in range(PASSES):
+            first = ps_s.tile([P, HALF], BF16, tag="s_ps")
+            k_transposes(0, g, first[:])
+            (nc.scalar.copy if g == 0 else nc.vector.tensor_copy)(out=k_t[:, g * HALF : (g + 1) * HALF], in_=first[:])
+        for half in range(2):
+            first = ps_s.tile([P, HALF], BF16, tag="s_ps")
+            q_transposes(0, half, first[:])
+            (nc.scalar.copy if half == 0 else nc.vector.tensor_copy)(out=q_t[:, half * HALF : (half + 1) * HALF], in_=first[:])
 
-        for k in range(-1, N_UNITS + 8):
-            group = (k - 1) // RING - 1
-            new_group = (k - 1) % RING == 0 and 0 <= group < N_UNITS // RING
+        last = N_UNITS - 1
+        for k in range(-2, last + 1):
             batch, phase = divmod(k, UNITS)
             nb = batch + 1
             prepare = k >= 0 and nb < B
-            if prepare and phase == 3:
-                q_copy(nb)
-            if 0 <= k + 1 < N_UNITS:
-                scores(k + 1)
-            if 1 <= batch < B and phase == 0:
-                mean_matmuls(batch)
-            if prepare and phase == 2:
-                q_transposes(nb)
-            if prepare and phase == 4:
-                k_transposes(nb)
-            if 0 <= k - 4 < N_UNITS and (k - 4) % 2 == 1:
-                pv_passes(k - 5)
-                pv_passes(k - 4)
-            if 0 <= k + 1 < N_UNITS:
-                row_max(k + 1)
-            if 0 <= k - 3 < N_UNITS and (k - 3) % 2 == 1:
-                e_quantise((k - 3) // 2)
-            if new_group:
-                row_sums(group)
+            if 0 <= batch + 2 < B and phase == 6 and batch >= 0:
+                q_copy(batch + 2, 0)
+            if 0 < batch and batch + 1 < B and phase == 0:
+                q_copy(batch + 1, 1)
+            if k == 1 or k == 3:
+                q_copy(1, k // 2)
+            if 0 <= batch < B and phase == 5:
+                mean_copy(batch)
+            if 0 <= k - 2 < N_UNITS:
+                copy_out(k - 2)
+            if prepare and (phase == 2 or phase == 4):
+                k_copy(nb, phase // 2 - 1)
+            if k % RING == 1 and 0 <= (k - 5) // RING < N_UNITS // RING:
+                row_sums((k - 5) // RING)
+            if 0 <= k + 2 < N_UNITS:
+                scores(k + 2)
+                row_max(k + 2, 0)
+                row_max(k + 2, 1)
+                exp_bias(k + 2)
+            if 0 <= batch < B and phase == 4:
+                mean_matmul(batch)
             if 0 <= k - 1 < N_UNITS:
                 e_transposes(k - 1)
-            if 0 <= k - 7 < N_UNITS and k % 2 == 1:
-                finish(k - 7)
-                finish(k - 6)
-            if 0 <= k + 1 < N_UNITS:
-                exp_bias(k + 1)
-            if new_group:
-                reciprocals(group)
-            if 0 <= k < N_UNITS:
+            if 0 <= k < last:
                 exps(k)
-            if 1 <= batch < B and phase == 0:
-                mean_copy(batch)
-            if prepare and phase == 4:
-                k_copy(nb)
-            if 0 <= k - 1 < N_UNITS:
-                copy_out(k - 1)
+            if k == last:
+                exps(k, (0,))
+            if 0 <= k - 5 < N_UNITS and k % 2 == 1:
+                pv_passes(k - 5)
+                pv_passes(k - 4)
             if k == 1:
-                mean_matmuls(0)
-                mean_copy(0)
                 v_quantise(0)
+            if 0 <= k - 3 < N_UNITS and k % 2 == 1:
+                e_quantise((k - 3) // 2)
+            if 0 <= k - 6 < N_UNITS and k % 2 == 0:
+                finish(k - 6)
+                finish(k - 5)
+            if 0 < batch < B and phase == 0:
+                v_quantise(batch)
+            if k % RING == 1 and 0 <= (k - 5) // RING < N_UNITS // RING:
+                reciprocals((k - 5) // RING)
+            if prepare and (phase == 1 or phase == 3):
+                k_transposes(nb, phase // 2, spare_16)
+            if k >= 0 and batch + 2 < B and (phase == 5 or phase == 7):
+                q_transposes(batch + 2, phase // 2 - 2, spare_16)
+            if k == 0 or k == 2:
+                q_transposes(1, k // 2, spare_16)
+            if k == -2:
+                for x in range(PIECES):
+                    v_regroup(0, x)
+            if k == -1:
+                for x in range(PIECES):
+                    pair_sum(0, x)
             if prepare:
                 if phase < PIECES:
                     v_regroup(nb, phase)
@@ -322,5 +360,35 @@ def tile_scaleddotproductattention_kernel(tc, query_in, key_in, value_in, out):
                     pair_sum(nb, phase - PIECES)
                 if phase == 0 and nb + 2 < B:
                     load(nb + 2)
-                if phase == 7:
-                    v_quantise(nb)
+            if 0 <= batch < B:
+                if phase == 0:
+                    piece_sum(batch, 0, 1)
+                if phase == 1:
+                    piece_sum(batch, 2, 3)
+                if phase == 2:
+                    piece_sum(batch, 0, 2)
+
+        copy_out(last - 1)
+        last_transposes(last, 0)
+        exps(last, (1,))
+        finish(last - 5)
+        finish(last - 4)
+        e_code = work.tile([P, 2 * PASSES * P], U32, align_bytes=64)
+        e_scale = work.tile([P, 2 * PASSES * P], U8, align_bytes=64)
+        e_codes[last // 2], e_scales[last // 2] = e_code, e_scale
+        last_copy(last, 0)
+        last_quantise(last - 1, 0, PASSES * P)
+        last_transposes(last, 1)
+        last_copy(last, 1)
+        pv_passes(last - 3)
+        pv_passes(last - 2)
+        row_sums(last // RING)
+        reciprocals(last // RING)
+        finish(last - 3)
+        finish(last - 2)
+        last_quantise(last, PASSES * P, 3 * P)
+        pv_passes(last - 1)
+        last_quantise(last, 3 * P, 4 * P)
+        pv_passes(last)
+        finish(last - 1)
+        finish(last)

@@ -24,7 +24,6 @@ RING = 4
 PIECES = 4
 WARM_UP = 4
 WORDS = 2
-VECTOR_HALVES = (0,)
 SCALE = 1.0 / math.sqrt(D)
 FLOPS = 4 * B * T * T * D
 
@@ -47,19 +46,19 @@ def tile_scaleddotproductattention_kernel(tc, query_in, key_in, value_in, out):
         masks.make_identity(nc, ident[:])
         ident_w = const.tile([P, P], F32)
         masks.make_identity(nc, ident_w[:])
-        mean_w = const.tile([P, P], F32)
-        nc.vector.memset(mean_w[:], 1.0 / T)
         bank = ps_pv.tile([P, 4, D], F32)
         pv = bank[:, 0:2, :]
         spare = bank[:, 2:4, :].rearrange("p s d -> p (s d)")
         spare_16 = spare.bitcast(BF16)
         idle_rhs = const.tile([P, HALF], BF16)
         nc.vector.memset(idle_rhs[:], 0.0)
+        twos = const.tile([P, P // 2], BF16)
+        nc.vector.tensor_tensor(out=twos[:], in0=ident[:, 0:P:2], in1=ident[:, 1:P:2], op=ALU.add)
 
-        q_raws, k_raws, v_raws = {}, {}, {}
-        q_ts, k_ts, v_codes, v_scales, means, pairs, v_grps, preps = {}, {}, {}, {}, {}, {}, {}, {}
-        s_tiles, biases, e_tiles, x_tiles, grps, e_codes, e_scales = {}, {}, {}, {}, {}, {}, {}
-        sums, totals, recips, results, maxes = {}, {}, {}, {}, {}
+        q_raws, k_raws, v_raws, v_rows = {}, {}, {}, {}
+        q_ts, k_ts, v_codes, v_scales, columns, means, v_grps = {}, {}, {}, {}, {}, {}, {}
+        s_tiles, maxes, biases, e_tiles, x_tiles, grps, e_codes, e_scales = {}, {}, {}, {}, {}, {}, {}, {}
+        sums, totals, recips, results = {}, {}, {}, {}
 
         def load(b):
             k_raw = raw.tile([P, 2 * PASSES, WORDS, D], BF16)
@@ -71,17 +70,20 @@ def tile_scaleddotproductattention_kernel(tc, query_in, key_in, value_in, out):
             nc.sync.dma_start(out=q_raw[:], in_=query_in[b].rearrange("(p i) d -> p i d", i=UNITS))
             v_raw = raw.tile([P, PASSES, PACK, D], BF16)
             nc.sync.dma_start(out=v_raw[:], in_=value_in[b].rearrange("(g p t) d -> p g t d", g=PASSES, t=PACK))
-            q_raws[b], k_raws[b], v_raws[b] = q_raw, k_raw, v_raw
+            v_row = raw.tile([P, UNITS, D], BF16)
+            nc.sync.dma_start(out=v_row[:], in_=value_in[b].rearrange("(x p) d -> p x d", p=P))
+            q_raws[b], k_raws[b], v_raws[b], v_rows[b] = q_raw, k_raw, v_raw, v_row
 
         def q_transposes(b, half, place):
             for i in range(4):
                 nc.tensor.transpose(place[:, i * P : (i + 1) * P], q_raws[b][:, half * 4 + i, :], ident[:])
 
-        def q_copy(b, half):
+        def q_copy(b, half, place):
             if half == 0:
                 q_t = opnd.tile([P, T], BF16)
                 q_ts[b] = q_t
-            nc.vector.tensor_copy(out=q_ts[b][:, half * HALF : (half + 1) * HALF], in_=spare_16)
+            cols = q_ts[b][:, half * HALF : (half + 1) * HALF]
+            nc.vector.tensor_copy(out=cols, in_=place)
 
         def k_transposes(b, g, place):
             for u in range(WORDS):
@@ -89,32 +91,35 @@ def tile_scaleddotproductattention_kernel(tc, query_in, key_in, value_in, out):
                     c = u * 2 + e
                     nc.tensor.transpose(place[:, c * P : (c + 1) * P], k_raws[b][:, g * 2 + e, u, :], ident[:])
 
-        def k_copy(b, g):
+        def k_copy(b, g, place):
             if g == 0:
                 k_t = opnd.tile([P, T], BF16)
                 k_ts[b] = k_t
-            out_cols = k_ts[b][:, g * HALF : (g + 1) * HALF]
-            if g in VECTOR_HALVES:
-                nc.vector.tensor_copy(out=out_cols, in_=spare_16)
+            cols = k_ts[b][:, g * HALF : (g + 1) * HALF]
+            if g in (1,):
+                nc.vector.tensor_copy(out=cols, in_=place)
             else:
-                nc.scalar.copy(out=out_cols, in_=spare_16)
+                nc.scalar.copy(out=cols, in_=place)
 
-        def pair_sum(b, x):
-            if x == 0:
-                pair = opnd.tile([P, PIECES, D], F32)
-                pairs[b] = pair
-            halves = v_raws[b][:].rearrange("p g (u e) d -> p (g u) e d", e=2)
-            nc.gpsimd.tensor_tensor(out=pairs[b][:, x, :], in0=halves[:, x, 0, :], in1=halves[:, x, 1, :], op=ALU.add)
+        def column_matmuls(b):
+            for x in range(UNITS):
+                nc.tensor.matmul(
+                    out=spare[:, 0 : P // 2], lhsT=v_rows[b][:, x, :], rhs=twos[:], start=(x == 0), stop=(x == UNITS - 1)
+                )
 
-        def piece_sum(b, x, y):
-            nc.gpsimd.tensor_tensor(out=pairs[b][:, x, :], in0=pairs[b][:, x, :], in1=pairs[b][:, y, :], op=ALU.add)
+        def column_copy(b):
+            column = opnd.tile([P, 1], F32)
+            nc.vector.tensor_reduce(out=column[:], in_=spare[:, 0 : P // 2], axis=AX.X, op=ALU.add)
+            columns[b] = column
 
-        def mean_matmul(b):
-            nc.tensor.matmul(out=spare[:, 0:D], lhsT=mean_w[:], rhs=pairs[b][:, 0, :], start=True, stop=True)
+        def mean_transpose(b):
+            nc.tensor.transpose(spare[:, 0:D], columns[b][:].to_broadcast([P, P]), ident_w[:])
 
         def mean_copy(b):
             mean = opnd.tile([P, D], F32)
-            nc.vector.tensor_copy(out=mean[:], in_=spare[:, 0:D])
+            nc.vector.tensor_scalar(
+                out=mean[:], in0=spare[:, 0:D], scalar1=1.0 / T, scalar2=0.0, op0=ALU.mult, op1=ALU.add
+            )
             means[b] = mean
 
         def v_regroup(b, x):
@@ -147,15 +152,19 @@ def tile_scaleddotproductattention_kernel(tc, query_in, key_in, value_in, out):
             for h in range(2):
                 s_ps = ps_s.tile([P, HALF], F32)
                 nc.tensor.matmul(
-                    out=s_ps[:], lhsT=q_ts[b][:, i * P : (i + 1) * P], rhs=k_ts[b][:, h * HALF : (h + 1) * HALF], start=True, stop=True
+                    out=s_ps[:],
+                    lhsT=q_ts[b][:, i * P : (i + 1) * P],
+                    rhs=k_ts[b][:, h * HALF : (h + 1) * HALF],
+                    start=True,
+                    stop=True,
                 )
                 s_tiles[(n, h)] = s_ps
 
-        def row_max(n, h):
-            if h == 0:
-                mx = small.tile([P, 2], F32)
-                maxes[n] = mx
-            nc.vector.tensor_reduce(out=maxes[n][:, h : h + 1], in_=s_tiles[(n, h)][:], axis=AX.X, op=ALU.max)
+        def row_max(n):
+            mx = small.tile([P, 2], F32)
+            for h in range(2):
+                nc.vector.tensor_reduce(out=mx[:, h : h + 1], in_=s_tiles[(n, h)][:], axis=AX.X, op=ALU.max)
+            maxes[n] = mx
 
         def exp_bias(n):
             mx = maxes[n]
@@ -294,39 +303,45 @@ def tile_scaleddotproductattention_kernel(tc, query_in, key_in, value_in, out):
             first = ps_s.tile([P, HALF], BF16, tag="s_ps")
             q_transposes(0, half, first[:])
             (nc.scalar.copy if half == 0 else nc.vector.tensor_copy)(out=q_t[:, half * HALF : (half + 1) * HALF], in_=first[:])
+        for x in range(PIECES):
+            v_regroup(0, x)
 
         last = N_UNITS - 1
         for k in range(-2, last + 1):
             batch, phase = divmod(k, UNITS)
             nb = batch + 1
-            prepare = k >= 0 and nb < B
-            if 0 <= batch + 2 < B and phase == 6 and batch >= 0:
-                q_copy(batch + 2, 0)
-            if 0 < batch and batch + 1 < B and phase == 0:
-                q_copy(batch + 1, 1)
-            if k == 1 or k == 3:
-                q_copy(1, k // 2)
-            if 0 <= batch < B and phase == 5:
+            if batch >= 0 and batch + 2 < B and phase == 6:
+                q_copy(batch + 2, 0, spare_16)
+            if batch >= 1 and batch + 1 < B and phase == 0:
+                q_copy(batch + 1, 1, spare_16)
+            if k == 3 or k == 5:
+                q_copy(1, k // 2 - 1, spare_16)
+            if 0 <= nb < B and phase == 7:
+                column_copy(nb)
+            if 0 <= batch < B and phase == 1:
                 mean_copy(batch)
+            if 0 <= nb < B and k >= 0 and (phase == 2 or phase == 4) and phase // 2 - 1 in (1,):
+                k_copy(nb, phase // 2 - 1, spare_16)
             if 0 <= k - 2 < N_UNITS:
                 copy_out(k - 2)
-            if prepare and (phase == 2 or phase == 4):
-                k_copy(nb, phase // 2 - 1)
             if k % RING == 1 and 0 <= (k - 5) // RING < N_UNITS // RING:
                 row_sums((k - 5) // RING)
             if 0 <= k + 2 < N_UNITS:
                 scores(k + 2)
-                row_max(k + 2, 0)
-                row_max(k + 2, 1)
+                row_max(k + 2)
                 exp_bias(k + 2)
-            if 0 <= batch < B and phase == 4:
-                mean_matmul(batch)
             if 0 <= k - 1 < N_UNITS:
                 e_transposes(k - 1)
+            if 0 <= nb < B and phase == 6:
+                column_matmuls(nb)
+            if 0 <= batch < B and phase == 0:
+                mean_transpose(batch)
             if 0 <= k < last:
                 exps(k)
             if k == last:
                 exps(k, (0,))
+            if 0 <= nb < B and k >= 0 and (phase == 2 or phase == 4) and phase // 2 - 1 not in (1,):
+                k_copy(nb, phase // 2 - 1, spare_16)
             if 0 <= k - 5 < N_UNITS and k % 2 == 1:
                 pv_passes(k - 5)
                 pv_passes(k - 4)
@@ -341,32 +356,16 @@ def tile_scaleddotproductattention_kernel(tc, query_in, key_in, value_in, out):
                 v_quantise(batch)
             if k % RING == 1 and 0 <= (k - 5) // RING < N_UNITS // RING:
                 reciprocals((k - 5) // RING)
-            if prepare and (phase == 1 or phase == 3):
+            if 0 <= nb < B and k >= 0 and (phase == 1 or phase == 3):
                 k_transposes(nb, phase // 2, spare_16)
             if k >= 0 and batch + 2 < B and (phase == 5 or phase == 7):
                 q_transposes(batch + 2, phase // 2 - 2, spare_16)
-            if k == 0 or k == 2:
-                q_transposes(1, k // 2, spare_16)
-            if k == -2:
-                for x in range(PIECES):
-                    v_regroup(0, x)
-            if k == -1:
-                for x in range(PIECES):
-                    pair_sum(0, x)
-            if prepare:
-                if phase < PIECES:
-                    v_regroup(nb, phase)
-                else:
-                    pair_sum(nb, phase - PIECES)
-                if phase == 0 and nb + 2 < B:
-                    load(nb + 2)
-            if 0 <= batch < B:
-                if phase == 0:
-                    piece_sum(batch, 0, 1)
-                if phase == 1:
-                    piece_sum(batch, 2, 3)
-                if phase == 2:
-                    piece_sum(batch, 0, 2)
+            if k == 2 or k == 4:
+                q_transposes(1, k // 2 - 1, spare_16)
+            if 0 <= nb < B and phase < PIECES and k >= 0:
+                v_regroup(nb, phase)
+            if k >= 0 and phase == 0 and nb + 2 < B:
+                load(nb + 2)
 
         copy_out(last - 1)
         last_transposes(last, 0)

@@ -58,7 +58,21 @@ def tile_scaleddotproductattention_kernel(tc, query_in, key_in, value_in, out):
         q_raws, k_raws, v_raws, v_rows = {}, {}, {}, {}
         q_ts, k_ts, v_codes, v_scales, columns, means, v_grps = {}, {}, {}, {}, {}, {}, {}
         s_tiles, maxes, biases, e_tiles, x_tiles, grps, e_codes, e_scales = {}, {}, {}, {}, {}, {}, {}, {}
-        sums, totals, recips, results = {}, {}, {}, {}
+        sums, totals, recips, results, last_pvs = {}, {}, {}, {}, {}
+
+        def load_first():
+            k_raw = raw.tile([P, 2 * PASSES, WORDS, D], BF16)
+            q_raw = raw.tile([P, UNITS, D], BF16)
+            k_rows = key_in[0].rearrange("(c a u e) d -> e a c u d", c=2 * PASSES, u=WORDS, e=2)
+            q_rows = query_in[0].rearrange("(p i) d -> p i d", i=UNITS)
+            nc.sync.dma_start(out=q_raw[:, 0:4, :], in_=q_rows[:, 0:4, :])
+            for g in range(PASSES):
+                c = slice(2 * g, 2 * g + 2)
+                for e in range(2):
+                    for u in range(WORDS):
+                        nc.sync.dma_start(out=k_raw[e:P:2, c, u, :], in_=k_rows[e, :, c, u, :])
+            nc.sync.dma_start(out=q_raw[:, 4:8, :], in_=q_rows[:, 4:8, :])
+            q_raws[0], k_raws[0] = q_raw, k_raw
 
         def load(b):
             k_raw = raw.tile([P, 2 * PASSES, WORDS, D], BF16)
@@ -68,11 +82,15 @@ def tile_scaleddotproductattention_kernel(tc, query_in, key_in, value_in, out):
                     nc.sync.dma_start(out=k_raw[e:P:2, :, u, :], in_=k_rows[e, :, :, u, :])
             q_raw = raw.tile([P, UNITS, D], BF16)
             nc.sync.dma_start(out=q_raw[:], in_=query_in[b].rearrange("(p i) d -> p i d", i=UNITS))
+            q_raws[b], k_raws[b] = q_raw, k_raw
+            load_v(b)
+
+        def load_v(b):
             v_raw = raw.tile([P, PASSES, PACK, D], BF16)
             nc.sync.dma_start(out=v_raw[:], in_=value_in[b].rearrange("(g p t) d -> p g t d", g=PASSES, t=PACK))
             v_row = raw.tile([P, UNITS, D], BF16)
             nc.sync.dma_start(out=v_row[:], in_=value_in[b].rearrange("(x p) d -> p x d", p=P))
-            q_raws[b], k_raws[b], v_raws[b], v_rows[b] = q_raw, k_raw, v_raw, v_row
+            v_raws[b], v_rows[b] = v_raw, v_row
 
         def q_transposes(b, half, place):
             for i in range(4):
@@ -240,14 +258,16 @@ def tile_scaleddotproductattention_kernel(tc, query_in, key_in, value_in, out):
             )
             e_codes[pair], e_scales[pair] = e_code, e_scale
 
+        def result_place(n):
+            return pv[:, n % 2, :] if n < N_UNITS - 2 else last_pvs[n][:]
+
         def pv_passes(n):
             b = n // UNITS
-            slot = n % 2
             for g in range(PASSES):
                 cols = slice(g * P, (g + 1) * P)
                 e_cols = slice((n % 2 * PASSES + g) * P, (n % 2 * PASSES + g + 1) * P)
                 nc.tensor.matmul_mx(
-                    out=pv[:, slot, :],
+                    out=result_place(n),
                     lhsT=e_codes[n // 2][:, e_cols].bitcast(FP8X4),
                     lhsT_scale=e_scales[n // 2][:, e_cols],
                     rhs=v_codes[b][:, cols].bitcast(FP8X4),
@@ -274,7 +294,7 @@ def tile_scaleddotproductattention_kernel(tc, query_in, key_in, value_in, out):
                 results[b] = res
             nc.vector.scalar_tensor_tensor(
                 out=results[b][:, i, :],
-                in0=pv[:, n % 2, :],
+                in0=result_place(n),
                 scalar=recips[j][:, slot : slot + 1],
                 in1=means[b][:],
                 op0=ALU.mult,
@@ -287,7 +307,9 @@ def tile_scaleddotproductattention_kernel(tc, query_in, key_in, value_in, out):
                 )
 
         ctx.enter_context(tc.manual_schedule())
-        for b in range(3):
+        load_first()
+        load_v(0)
+        for b in range(1, 3):
             load(b)
         for w in range(WARM_UP):
             idle_ps = ps_s.tile([P, HALF], F32, tag="s_ps")
@@ -295,14 +317,13 @@ def tile_scaleddotproductattention_kernel(tc, query_in, key_in, value_in, out):
         k_t = opnd.tile([P, T], BF16)
         q_t = opnd.tile([P, T], BF16)
         k_ts[0], q_ts[0] = k_t, q_t
+        first = ps_s.tile([P, HALF], BF16, tag="s_ps")
+        q_transposes(0, 0, first[:])
+        nc.vector.tensor_copy(out=q_t[:, 0:HALF], in_=first[:])
         for g in range(PASSES):
             first = ps_s.tile([P, HALF], BF16, tag="s_ps")
             k_transposes(0, g, first[:])
             (nc.scalar.copy if g == 0 else nc.vector.tensor_copy)(out=k_t[:, g * HALF : (g + 1) * HALF], in_=first[:])
-        for half in range(2):
-            first = ps_s.tile([P, HALF], BF16, tag="s_ps")
-            q_transposes(0, half, first[:])
-            (nc.scalar.copy if half == 0 else nc.vector.tensor_copy)(out=q_t[:, half * HALF : (half + 1) * HALF], in_=first[:])
         for x in range(PIECES):
             v_regroup(0, x)
 
@@ -330,6 +351,10 @@ def tile_scaleddotproductattention_kernel(tc, query_in, key_in, value_in, out):
                 scores(k + 2)
                 row_max(k + 2)
                 exp_bias(k + 2)
+            if k == -2:
+                first = ps_x.tile([P, HALF], BF16, tag="xt")
+                q_transposes(0, 1, first[:])
+                nc.scalar.copy(out=q_t[:, HALF:T], in_=first[:])
             if 0 <= k - 1 < N_UNITS:
                 e_transposes(k - 1)
             if 0 <= nb < B and phase == 6:
@@ -377,17 +402,18 @@ def tile_scaleddotproductattention_kernel(tc, query_in, key_in, value_in, out):
         e_codes[last // 2], e_scales[last // 2] = e_code, e_scale
         last_copy(last, 0)
         last_quantise(last - 1, 0, PASSES * P)
+        last_quantise(last, PASSES * P, 3 * P)
         last_transposes(last, 1)
         last_copy(last, 1)
         pv_passes(last - 3)
         pv_passes(last - 2)
         row_sums(last // RING)
         reciprocals(last // RING)
-        finish(last - 3)
-        finish(last - 2)
-        last_quantise(last, PASSES * P, 3 * P)
+        for n in range(last - 1, last + 1):
+            last_pv = ps_s.tile([P, D], F32, tag="s_ps")
+            last_pvs[n] = last_pv
         pv_passes(last - 1)
         last_quantise(last, 3 * P, 4 * P)
         pv_passes(last)
-        finish(last - 1)
-        finish(last)
+        for n in range(last - 3, last + 1):
+            finish(n)

@@ -187,7 +187,7 @@ def tile_scaleddotproductattention_kernel(tc, query_in, key_in, value_in, out):
         def exp_bias(n):
             mx = maxes[n]
             bias = small.tile([P, 1], F32)
-            (nc.vector if n < 2 else nc.gpsimd).tensor_scalar(
+            (nc.vector if n < 3 else nc.gpsimd).tensor_scalar(
                 out=bias[:], in0=mx[:, 0:1], scalar1=mx[:, 1:2], scalar2=-SCALE, op0=ALU.max, op1=ALU.mult
             )
             biases[n] = bias
@@ -377,7 +377,7 @@ def tile_scaleddotproductattention_kernel(tc, query_in, key_in, value_in, out):
             if 0 <= k - 6 < N_UNITS and k % 2 == 0:
                 finish(k - 6)
                 finish(k - 5)
-            if 0 < batch < B and phase == 0:
+            if 0 < batch < B and phase == 2:
                 v_quantise(batch)
             if k % RING == 1 and 0 <= (k - 5) // RING < N_UNITS // RING:
                 reciprocals((k - 5) // RING)

import math
from contextlib import ExitStack

import concourse.masks as masks
import concourse.mybir as mybir

F32 = mybir.dt.float32
BF16 = mybir.dt.bfloat16
U32 = mybir.dt.uint32
U8 = mybir.dt.uint8
FP8X4 = mybir.dt.float8_e4m3fn_x4
ALU = mybir.AluOpType
ACT = mybir.ActivationFunctionType
AX = mybir.AxisListType

B, T, D = 16, 1024, 128
P = 128
PACK = 4
PASSES = T // (P * PACK)
UNITS = T // P
HALF = 512
N_UNITS = B * UNITS
RING = 4
PIECES = 4
WARM_UP = 4
WORDS = 2
SCALE = 1.0 / math.sqrt(D)
FLOPS = 4 * B * T * T * D


def tile_scaleddotproductattention_kernel(tc, query_in, key_in, value_in, out):
    nc = tc.nc
    with ExitStack() as ctx:
        const = ctx.enter_context(tc.tile_pool(name="const", bufs=1))
        raw = ctx.enter_context(tc.tile_pool(name="raw", bufs=3))
        opnd = ctx.enter_context(tc.tile_pool(name="opnd", bufs=3))
        work = ctx.enter_context(tc.tile_pool(name="work", bufs=3))
        grouped = ctx.enter_context(tc.tile_pool(name="grouped", bufs=3))
        small = ctx.enter_context(tc.tile_pool(name="small", bufs=4))
        outp = ctx.enter_context(tc.tile_pool(name="outp", bufs=2))
        ps_s = ctx.enter_context(tc.psum_pool(name="ps_s", bufs=6))
        ps_x = ctx.enter_context(tc.psum_pool(name="ps_x", bufs=1))
        ps_pv = ctx.enter_context(tc.psum_pool(name="ps_pv", bufs=1))

        ident = const.tile([P, P], BF16)
        masks.make_identity(nc, ident[:])
        ident_w = const.tile([P, P], F32)
        masks.make_identity(nc, ident_w[:])
        bank = ps_pv.tile([P, 4, D], F32)
        pv = bank[:, 0:2, :]
        spare = bank[:, 2:4, :].rearrange("p s d -> p (s d)")
        spare_16 = spare.bitcast(BF16)
        idle_rhs = const.tile([P, HALF], BF16)
        nc.vector.memset(idle_rhs[:], 0.0)
        twos = const.tile([P, P // 2], BF16)
        nc.vector.tensor_tensor(out=twos[:], in0=ident[:, 0:P:2], in1=ident[:, 1:P:2], op=ALU.add)

        q_raws, k_raws, v_raws, v_rows = {}, {}, {}, {}
        q_ts, k_ts, v_codes, v_scales, columns, means, v_grps = {}, {}, {}, {}, {}, {}, {}
        s_tiles, maxes, biases, e_tiles, x_tiles, grps, e_codes, e_scales = {}, {}, {}, {}, {}, {}, {}, {}
        sums, totals, recips, results, last_pvs = {}, {}, {}, {}, {}

        def load_first():
            k_raw = raw.tile([P, 2 * PASSES, WORDS, D], BF16)
            q_raw = raw.tile([P, UNITS, D], BF16)
            k_rows = key_in[0].rearrange("(c a u e) d -> e a c u d", c=2 * PASSES, u=WORDS, e=2)
            q_rows = query_in[0].rearrange("(p i) d -> p i d", i=UNITS)
            nc.sync.dma_start(out=q_raw[:, 0:4, :], in_=q_rows[:, 0:4, :])
            for g in range(PASSES):
                c = slice(2 * g, 2 * g + 2)
                for e in range(2):
                    for u in range(WORDS):
                        nc.sync.dma_start(out=k_raw[e:P:2, c, u, :], in_=k_rows[e, :, c, u, :])
            nc.sync.dma_start(out=q_raw[:, 4:8, :], in_=q_rows[:, 4:8, :])
            q_raws[0], k_raws[0] = q_raw, k_raw

        def load(b):
            k_raw = raw.tile([P, 2 * PASSES, WORDS, D], BF16)
            k_rows = key_in[b].rearrange("(c a u e) d -> e a c u d", c=2 * PASSES, u=WORDS, e=2)
            for e in range(2):
                for u in range(WORDS):
                    nc.sync.dma_start(out=k_raw[e:P:2, :, u, :], in_=k_rows[e, :, :, u, :])
            q_raw = raw.tile([P, UNITS, D], BF16)
            nc.sync.dma_start(out=q_raw[:], in_=query_in[b].rearrange("(p i) d -> p i d", i=UNITS))
            q_raws[b], k_raws[b] = q_raw, k_raw
            load_v(b)

        def load_v(b):
            v_raw = raw.tile([P, PASSES, PACK, D], BF16)
            nc.sync.dma_start(out=v_raw[:], in_=value_in[b].rearrange("(g p t) d -> p g t d", g=PASSES, t=PACK))
            v_row = raw.tile([P, UNITS, D], BF16)
            nc.sync.dma_start(out=v_row[:], in_=value_in[b].rearrange("(x p) d -> p x d", p=P))
            v_raws[b], v_rows[b] = v_raw, v_row

        def q_transposes(b, half, place):
            for i in range(4):
                nc.tensor.transpose(place[:, i * P : (i + 1) * P], q_raws[b][:, half * 4 + i, :], ident[:])

        def q_copy(b, half, place):
            if half == 0:
                q_t = opnd.tile([P, T], BF16)
                q_ts[b] = q_t
            cols = q_ts[b][:, half * HALF : (half + 1) * HALF]
            nc.vector.tensor_copy(out=cols, in_=place)

        def k_transposes(b, g, place):
            for u in range(WORDS):
                for e in range(2):
                    c = u * 2 + e
                    nc.tensor.transpose(place[:, c * P : (c + 1) * P], k_raws[b][:, g * 2 + e, u, :], ident[:])

        def k_copy(b, g, place):
            if g == 0:
                k_t = opnd.tile([P, T], BF16)
                k_ts[b] = k_t
            cols = k_ts[b][:, g * HALF : (g + 1) * HALF]
            if g in (1,):
                nc.vector.tensor_copy(out=cols, in_=place)
            else:
                nc.scalar.copy(out=cols, in_=place)

        def column_matmuls(b):
            for x in range(UNITS):
                nc.tensor.matmul(
                    out=spare[:, 0 : P // 2], lhsT=v_rows[b][:, x, :], rhs=twos[:], start=(x == 0), stop=(x == UNITS - 1)
                )

        def column_copy(b):
            column = opnd.tile([P, 1], F32)
            nc.vector.tensor_reduce(out=column[:], in_=spare[:, 0 : P // 2], axis=AX.X, op=ALU.add)
            columns[b] = column

        def mean_transpose(b):
            nc.tensor.transpose(spare[:, 0:D], columns[b][:].to_broadcast([P, P]), ident_w[:])

        def mean_copy(b):
            mean = opnd.tile([P, D], F32)
            nc.vector.tensor_scalar(
                out=mean[:], in0=spare[:, 0:D], scalar1=1.0 / T, scalar2=0.0, op0=ALU.mult, op1=ALU.add
            )
            means[b] = mean

        def v_regroup(b, x):
            if x == 0:
                v_grp = opnd.tile([P, PASSES, D, PACK], BF16, align_bytes=64)
                v_grps[b] = v_grp
            g, half = divmod(x, 2)
            cols = slice(half * (D // 2), (half + 1) * (D // 2))
            nc.gpsimd.tensor_scalar(
                out=v_grps[b][:, g, cols, :],
                in0=v_raws[b][:, g, :, cols].rearrange("p t d -> p d t"),
                scalar1=1.0,
                scalar2=0.0,
                op0=ALU.mult,
                op1=ALU.add,
            )

        def v_quantise(b):
            v_code = opnd.tile([P, PASSES * D], U32, align_bytes=64)
            v_scale = opnd.tile([P, PASSES * D], U8, align_bytes=64)
            nc.vector.quantize_mx(
                out=v_code[:].bitcast(FP8X4),
                scales=v_scale[:],
                in_=v_grps[b][:].rearrange("p g d t -> p (g d t)"),
            )
            v_codes[b], v_scales[b] = v_code, v_scale

        def scores(n):
            b, i = divmod(n, UNITS)
            for h in range(2):
                s_ps = ps_s.tile([P, HALF], F32)
                nc.tensor.matmul(
                    out=s_ps[:],
                    lhsT=q_ts[b][:, i * P : (i + 1) * P],
                    rhs=k_ts[b][:, h * HALF : (h + 1) * HALF],
                    start=True,
                    stop=True,
                )
                s_tiles[(n, h)] = s_ps

        def row_max(n):
            mx = small.tile([P, 2], F32)
            for h in range(2):
                nc.vector.tensor_reduce(out=mx[:, h : h + 1], in_=s_tiles[(n, h)][:], axis=AX.X, op=ALU.max)
            maxes[n] = mx

        def exp_bias(n):
            mx = maxes[n]
            bias = small.tile([P, 1], F32)
            (nc.vector if n < 3 else nc.gpsimd).tensor_scalar(
                out=bias[:], in0=mx[:, 0:1], scalar1=mx[:, 1:2], scalar2=-SCALE, op0=ALU.max, op1=ALU.mult
            )
            biases[n] = bias

        def exps(n, halves=(0, 1)):
            j, slot = divmod(n, RING)
            if slot == 0 and 0 in halves:
                rs = small.tile([P, RING, 2], F32)
                sums[j] = rs
            if 0 in halves:
                e_sb = work.tile([P, T], BF16)
                e_tiles[n] = e_sb
            for h in halves:
                nc.scalar.activation(
                    out=e_tiles[n][:, h * HALF : (h + 1) * HALF],
                    in_=s_tiles[(n, h)][:],
                    func=ACT.Exp,
                    bias=biases[n][:],
                    scale=SCALE,
                    accum_out=sums[j][:, slot, h : h + 1],
                )

        def e_transposes(n):
            xt = ps_x.tile([P, PASSES * WORDS, P], F32)
            words = e_tiles[n][:].bitcast(F32)
            for c in range(PASSES * WORDS):
                nc.tensor.transpose(xt[:, c, :], words[:, c * P : (c + 1) * P], ident_w[:])
            x_tiles[n] = xt

        def last_transposes(n, g):
            xh = ps_s.tile([P, WORDS, P], F32, tag="s_ps")
            words = e_tiles[n][:].bitcast(F32)
            for u in range(WORDS):
                c = g * WORDS + u
                nc.tensor.transpose(xh[:, u, :], words[:, c * P : (c + 1) * P], ident_w[:])
            x_tiles[(n, g)] = xh

        def last_copy(n, g):
            lo = (n % 2) * T + g * HALF
            out_words = grps[n // 2][:, lo : lo + HALF].bitcast(F32).rearrange("p (q u) -> p q u", u=WORDS)
            (nc.vector.tensor_copy if g == 0 else nc.scalar.copy)(out=out_words, in_=x_tiles[(n, g)][:].rearrange("p u q -> p q u"))

        def last_quantise(n, lo, hi):
            nc.vector.quantize_mx(
                out=e_codes[n // 2][:, lo:hi].bitcast(FP8X4),
                scales=e_scales[n // 2][:, lo:hi],
                in_=grps[n // 2][:, PACK * lo : PACK * hi],
            )

        def copy_out(n):
            if n % 2 == 0:
                grp = grouped.tile([P, 2 * T], BF16, align_bytes=64)
                grps[n // 2] = grp
            (nc.vector.tensor_copy if n == N_UNITS - 2 else nc.scalar.copy)(
                out=grps[n // 2][:, (n % 2) * T : (n % 2 + 1) * T]
                .bitcast(F32)
                .rearrange("p (g q u) -> p g q u", g=PASSES, u=WORDS),
                in_=x_tiles[n][:].rearrange("p (g u) q -> p g q u", g=PASSES),
            )

        def e_quantise(pair):
            e_code = work.tile([P, 2 * PASSES * P], U32, align_bytes=64)
            e_scale = work.tile([P, 2 * PASSES * P], U8, align_bytes=64)
            nc.vector.quantize_mx(
                out=e_code[:].bitcast(FP8X4),
                scales=e_scale[:],
                in_=grps[pair][:],
            )
            e_codes[pair], e_scales[pair] = e_code, e_scale

        def result_place(n):
            return pv[:, n % 2, :] if n < N_UNITS - 2 else last_pvs[n][:]

        def pv_passes(n):
            b = n // UNITS
            for g in range(PASSES):
                cols = slice(g * P, (g + 1) * P)
                e_cols = slice((n % 2 * PASSES + g) * P, (n % 2 * PASSES + g + 1) * P)
                nc.tensor.matmul_mx(
                    out=result_place(n),
                    lhsT=e_codes[n // 2][:, e_cols].bitcast(FP8X4),
                    lhsT_scale=e_scales[n // 2][:, e_cols],
                    rhs=v_codes[b][:, cols].bitcast(FP8X4),
                    rhs_scale=v_scales[b][:, cols],
                    start=(g == 0),
                    stop=(g == PASSES - 1),
                )

        def row_sums(j):
            total = small.tile([P, RING], F32)
            nc.gpsimd.tensor_tensor(out=total[:], in0=sums[j][:, :, 0], in1=sums[j][:, :, 1], op=ALU.add)
            totals[j] = total

        def reciprocals(j):
            recip = small.tile([P, RING], F32)
            nc.vector.reciprocal(out=recip[:], in_=totals[j][:])
            recips[j] = recip

        def finish(n):
            b, i = divmod(n, UNITS)
            j, slot = divmod(n, RING)
            if i == 0:
                res = outp.tile([P, UNITS, D], F32)
                results[b] = res
            nc.vector.scalar_tensor_tensor(
                out=results[b][:, i, :],
                in0=result_place(n),
                scalar=recips[j][:, slot : slot + 1],
                in1=means[b][:],
                op0=ALU.mult,
                op1=ALU.subtract,
            )
            if n % 2 == 1 or n >= N_UNITS - 2:
                rows = slice(i - 1 if n < N_UNITS - 2 else i, i + 1)
                nc.sync.dma_start(
                    out=out[b].rearrange("(p i) d -> p i d", i=UNITS)[:, rows, :], in_=results[b][:, rows, :]
                )

        ctx.enter_context(tc.manual_schedule())
        load_first()
        load_v(0)
        for b in range(1, 3):
            load(b)
        for w in range(WARM_UP):
            idle_ps = ps_s.tile([P, HALF], F32, tag="s_ps")
            nc.tensor.matmul(out=idle_ps[:], lhsT=ident[:], rhs=idle_rhs[:], start=True, stop=True)
        k_t = opnd.tile([P, T], BF16)
        q_t = opnd.tile([P, T], BF16)
        k_ts[0], q_ts[0] = k_t, q_t
        first = ps_s.tile([P, HALF], BF16, tag="s_ps")
        q_transposes(0, 0, first[:])
        nc.vector.tensor_copy(out=q_t[:, 0:HALF], in_=first[:])
        for g in range(PASSES):
            first = ps_s.tile([P, HALF], BF16, tag="s_ps")
            k_transposes(0, g, first[:])
            (nc.scalar.copy if g == 0 else nc.vector.tensor_copy)(out=k_t[:, g * HALF : (g + 1) * HALF], in_=first[:])
        for x in range(PIECES):
            v_regroup(0, x)

        last = N_UNITS - 1
        for k in range(-2, last + 1):
            batch, phase = divmod(k, UNITS)
            nb = batch + 1
            if batch >= 0 and batch + 2 < B and phase == 6:
                q_copy(batch + 2, 0, spare_16)
            if batch >= 1 and batch + 1 < B and phase == 0:
                q_copy(batch + 1, 1, spare_16)
            if k == 3 or k == 5:
                q_copy(1, k // 2 - 1, spare_16)
            if 0 <= nb < B and phase == 7:
                column_copy(nb)
            if 0 <= batch < B and phase == 1:
                mean_copy(batch)
            if 0 <= nb < B and k >= 0 and (phase == 2 or phase == 4) and phase // 2 - 1 in (1,):
                k_copy(nb, phase // 2 - 1, spare_16)
            if 0 <= k - 2 < N_UNITS:
                copy_out(k - 2)
            if k % RING == 1 and 0 <= (k - 5) // RING < N_UNITS // RING:
                row_sums((k - 5) // RING)
            if 0 <= k + 2 < N_UNITS:
                scores(k + 2)
                row_max(k + 2)
                exp_bias(k + 2)
            if k == -2:
                first = ps_x.tile([P, HALF], BF16, tag="xt")
                q_transposes(0, 1, first[:])
                nc.scalar.copy(out=q_t[:, HALF:T], in_=first[:])
            if 0 <= k - 1 < N_UNITS:
                e_transposes(k - 1)
            if 0 <= nb < B and phase == 6:
                column_matmuls(nb)
            if 0 <= batch < B and phase == 0:
                mean_transpose(batch)
            if 0 <= k < last:
                exps(k)
            if k == last:
                exps(k, (0,))
            if 0 <= nb < B and k >= 0 and (phase == 2 or phase == 4) and phase // 2 - 1 not in (1,):
                k_copy(nb, phase // 2 - 1, spare_16)
            if 0 <= k - 5 < N_UNITS and k % 2 == 1:
                pv_passes(k - 5)
                pv_passes(k - 4)
            if k == 1:
                v_quantise(0)
            if 0 <= k - 3 < N_UNITS and k % 2 == 1:
                e_quantise((k - 3) // 2)
            if 0 <= k - 6 < N_UNITS and k % 2 == 0:
                finish(k - 6)
                finish(k - 5)
            if 0 < batch < B and phase == 2:
                v_quantise(batch)
            if k % RING == 1 and 0 <= (k - 5) // RING < N_UNITS // RING:
                reciprocals((k - 5) // RING)
            if 0 <= nb < B and k >= 0 and (phase == 1 or phase == 3):
                k_transposes(nb, phase // 2, spare_16)
            if k >= 0 and batch + 2 < B and (phase == 5 or phase == 7):
                q_transposes(batch + 2, phase // 2 - 2, spare_16)
            if k == 2 or k == 4:
                q_transposes(1, k // 2 - 1, spare_16)
            if 0 <= nb < B and phase < PIECES and k >= 0:
                v_regroup(nb, phase)
            if k >= 0 and phase == 0 and nb + 2 < B:
                load(nb + 2)

        copy_out(last - 1)
        last_transposes(last, 0)
        exps(last, (1,))
        finish(last - 5)
        finish(last - 4)
        e_code = work.tile([P, 2 * PASSES * P], U32, align_bytes=64)
        e_scale = work.tile([P, 2 * PASSES * P], U8, align_bytes=64)
        e_codes[last // 2], e_scales[last // 2] = e_code, e_scale
        last_copy(last, 0)
        last_quantise(last - 1, 0, PASSES * P)
        last_quantise(last, PASSES * P, 3 * P)
        last_transposes(last, 1)
        last_copy(last, 1)
        pv_passes(last - 3)
        pv_passes(last - 2)
        row_sums(last // RING)
        reciprocals(last // RING)
        for n in range(last - 1, last + 1):
            last_pv = ps_s.tile([P, D], F32, tag="s_ps")
            last_pvs[n] = last_pv
        pv_passes(last - 1)
        last_quantise(last, 3 * P, 4 * P)
        pv_passes(last)
        for n in range(last - 3, last + 1):
            finish(n)
